import numpy as np
import ml_dtypes


def mxq(x, axis, fmt="e4m3"):
    dtype, down = {"e4m3": (ml_dtypes.float8_e4m3fn, 7), "e5m2": (ml_dtypes.float8_e5m2, 14)}[fmt]
    v = np.moveaxis(np.asarray(x, np.float32).astype(ml_dtypes.bfloat16).astype(np.float64), axis, -1)
    blocks = v.reshape(v.shape[:-1] + (-1, 32))
    amax = np.abs(blocks).max(-1, keepdims=True)
    byte = np.maximum(np.where(amax > 0, np.frexp(amax)[1] - 1 + 127, 0) - down, 1)
    scale = np.exp2(byte - 127.0)
    codes = (blocks / scale).astype(np.float32).astype(dtype).astype(np.float64)
    return np.moveaxis((codes * scale).reshape(v.shape), -1, axis)


WIDE = False


def mx_kscale(k):
    if not WIDE:
        return np.ones(k)
    levels = np.array([10, -10, 5, -5, 0])
    if k % 512:
        return np.exp2(np.random.permutation(np.resize(levels, k // 32))).repeat(32)
    a = np.empty((k // 512, 16))
    for p in range(k // 512):
        a[p, :8] = np.random.permutation(np.resize(levels, 8))
        for g in range(8):
            far = levels[np.abs(levels - a[p, g]) >= 10]
            a[p, g + 8] = far[np.random.randint(len(far))]
    return np.exp2(a.ravel()).repeat(32)


BF16 = ml_dtypes.bfloat16


def bf(x):
    return np.asarray(x, np.float32).astype(BF16)


def f64(x):
    return np.asarray(x).astype(np.float64)


E2M1 = np.array([0.0, 0.5, 1.0, 1.5, 2.0, 3.0, 4.0, 6.0, -0.0, -0.5, -1.0, -1.5, -2.0, -3.0, -4.0, -6.0])


def pack_weight(w, fmt):
    k, n = w.shape
    w = f64(bf(w)).reshape(k // 32, 32, n)
    amax = np.abs(w).max(1)
    if fmt == "e4m3":
        byte = np.frexp(amax)[1] - 1 + 127 - 7
    else:
        mant, ex = np.frexp(amax / 6.0)
        byte = np.where(mant > 0.5, ex, ex - 1) + 127
    byte = np.clip(np.where(amax > 0, byte, 1), 1, 254)
    scaled = (w * np.exp2(127.0 - byte)[:, None, :]).reshape(k, n).astype(np.float32)
    by_word = np.ascontiguousarray(scaled.reshape(k // 512, 128, 4, n).transpose(0, 1, 3, 2))
    if fmt == "e4m3":
        words = by_word.astype(ml_dtypes.float8_e4m3fn).view(np.uint8)
    else:
        c = by_word.astype(ml_dtypes.float4_e2m1fn).view(np.uint8) & 0xF
        words = c[..., 0::2] | (c[..., 1::2] << 4)
    return np.ascontiguousarray(words), np.ascontiguousarray(byte.astype(np.uint8).reshape(k // 512, 16, n))


def unpack_weight(words, scales, fmt):
    g, p, n, _ = words.shape
    if fmt == "e4m3":
        vals = np.ascontiguousarray(words).view(ml_dtypes.float8_e4m3fn).astype(np.float64)
    else:
        nib = np.empty((g, p, n, 4), np.uint8)
        nib[..., 0::2] = words & 0xF
        nib[..., 1::2] = words >> 4
        vals = E2M1[nib]
    vals = vals * np.repeat(np.exp2(scales.astype(np.float64) - 127.0), 8, axis=1)[..., None]
    return vals.transpose(0, 1, 3, 2).reshape(g * 512, n)


B, T, C, N_HEAD, N_KV, D_LAT, D_ROPE = 2, 2048, 1024, 8, 4, 512, 64
HD = C // N_HEAD
D_NOPE = HD - D_ROPE
DR2 = D_ROPE // 2
ROPE_BASE = 10000.0
EPS = 1.1920928955078125e-07


def rope_tables():
    half = HD // 2
    inv_freq = 1.0 / (ROPE_BASE ** (np.arange(half) / half))
    ang = np.arange(T)[:, None] * inv_freq[None, :DR2]
    return np.cos(ang), np.sin(ang)


def rms(u):
    return u * (1.0 / np.sqrt(np.mean(u * u, axis=-1, keepdims=True) + EPS))


def draw0():
    s, t = mx_kscale(C), mx_kscale(D_LAT)
    cos, sin = rope_tables()
    x = bf(np.random.standard_normal((B, T, C)) * s)
    w_kv_words, w_kv_scales = pack_weight(np.random.standard_normal((C, D_LAT)) / np.sqrt(C) / s[:, None] * t, "e4m3")
    w_kup_words, w_kup_scales = pack_weight(np.random.standard_normal((D_LAT, N_KV * D_NOPE)) / np.sqrt(D_LAT) / t[:, None], "e4m3")
    w_vup_words, w_vup_scales = pack_weight(np.random.standard_normal((D_LAT, N_KV * HD)) / np.sqrt(D_LAT) / t[:, None], "e4m3")
    w_krope_words, w_krope_scales = pack_weight(np.random.standard_normal((C, N_KV * D_ROPE)) / np.sqrt(C) / s[:, None], "e4m3")
    return {"x": x,
            "cos": bf(cos), "sin": bf(sin),
            "w_kv_words": w_kv_words, "w_kv_scales": w_kv_scales,
            "w_kup_words": w_kup_words, "w_kup_scales": w_kup_scales,
            "w_vup_words": w_vup_words, "w_vup_scales": w_vup_scales,
            "w_krope_words": w_krope_words, "w_krope_scales": w_krope_scales}


def core(x, cos, sin, w_kv_words, w_kv_scales, w_kup_words, w_kup_scales, w_vup_words, w_vup_scales, w_krope_words, w_krope_scales):
    xq = mxq(f64(x), 2, "e4m3")
    latent = xq @ unpack_weight(w_kv_words, w_kv_scales, "e4m3")
    lq = mxq(latent, 2, "e4m3")
    k_nope = (lq @ unpack_weight(w_kup_words, w_kup_scales, "e4m3")).reshape(B, T, N_KV, D_NOPE)
    r = (xq @ unpack_weight(w_krope_words, w_krope_scales, "e4m3")).reshape(B, T, N_KV, D_ROPE)
    c, sn = f64(cos)[None, :, None, :], f64(sin)[None, :, None, :]
    r1, r2 = r[..., :DR2], r[..., DR2:]
    k_rope = np.concatenate([r1 * c + r2 * sn, -r1 * sn + r2 * c], axis=-1)
    k = rms(np.concatenate([k_rope, k_nope], axis=-1))
    v = (lq @ unpack_weight(w_vup_words, w_vup_scales, "e4m3")).reshape(B, T, N_KV, HD)
    return k, v


def e4m3fn_bytes(y):
    return np.clip(np.asarray(y, np.float64), -448.0, 448.0).astype(np.float32).astype(ml_dtypes.float8_e4m3fn).view(np.uint8)


def e4m3fn_values(b):
    return np.asarray(b, np.uint8).view(ml_dtypes.float8_e4m3fn).astype(np.float64)


def setup_inputs():
    d = draw0()
    x0 = np.asarray(d['x']).astype(np.float64)
    s = (np.max(np.abs(x0), axis=(0, 1), keepdims=True) / 448.0).astype(np.float32)
    out = {}
    for k, v in d.items():
        if k == 'x':
            out['x_bytes'] = e4m3fn_bytes(x0 / s.astype(np.float64))
            out['x_scale'] = s
        else:
            out[k] = v
    return out


def reference(x_bytes, x_scale, cos, sin, w_kv_words, w_kv_scales, w_kup_words, w_kup_scales, w_vup_words, w_vup_scales, w_krope_words, w_krope_scales):
    return core(e4m3fn_values(x_bytes) * x_scale.astype(np.float64), cos, sin, w_kv_words, w_kv_scales, w_kup_words, w_kup_scales, w_vup_words, w_vup_scales, w_krope_words, w_krope_scales)

@@ -1,0 +1,328 @@
+from contextlib import ExitStack
+
+import concourse.mybir as mybir
+from concourse.masks import make_identity
+
+B, T, C, DL = 2, 2048, 1024, 512
+NKV, HD, DR, DN = 4, 128, 64, 64
+TOK = B * T
+EPS = 1.1920928955078125e-07
+FLOPS = 2 * TOK * (C * DL + DL * NKV * DN + DL * NKV * HD + C * NKV * DR)
+
+F32 = mybir.dt.float32
+BF16 = mybir.dt.bfloat16
+I32 = mybir.dt.int32
+U32 = mybir.dt.uint32
+U8 = mybir.dt.uint8
+FP8 = mybir.dt.float8_e4m3fn
+FP8X4 = mybir.dt.float8_e4m3fn_x4
+ACT = mybir.ActivationFunctionType
+ALU = mybir.AluOpType
+
+P = 128
+RUN = 4
+NT = TOK // P
+NLOAD = NT // RUN
+BUFS = dict(xs=6, xg=4, xq=6, lg=4, lq=4, pr=4, kc=6, ko=4, vo=4, ss=6, junk=6)
+
+
+def tile_mlacausalselfattention_pa_t_w8_kernel(
+    tc, x_bytes, x_scale, cos, sin, w_kv_words, w_kv_scales, w_kup_words, w_kup_scales,
+    w_vup_words, w_vup_scales, w_krope_words, w_krope_scales, out_k, out_v,
+):
+    nc = tc.nc
+    x_v = x_bytes.rearrange("b t k -> (b t) k").rearrange("(s p i) k -> s p i k", p=P, i=RUN)
+    k_v = out_k.rearrange("b t h d -> (b t) (h d)").rearrange("(s p i) c -> s i p c", p=P, i=RUN)
+    v_v = out_v.rearrange("b t h d -> (b t) (h d)").rearrange("(s p i) c -> s i p c", p=P, i=RUN)
+
+    with ExitStack() as ctx:
+        keep = ctx.enter_context(tc.tile_pool(name="keep", bufs=1))
+        xin = ctx.enter_context(tc.tile_pool(name="xin", bufs=NLOAD))
+        pools = {}
+        for name, bufs in BUFS.items():
+            pools[name] = ctx.enter_context(tc.tile_pool(name=name, bufs=bufs))
+        ps_x = ctx.enter_context(tc.psum_pool(name="ps_x", bufs=2))
+        ps_l = ctx.enter_context(tc.psum_pool(name="ps_l", bufs=2))
+        ps_r = ctx.enter_context(tc.psum_pool(name="ps_r", bufs=1))
+        ps_n = ctx.enter_context(tc.psum_pool(name="ps_n", bufs=1))
+        ps_v = ctx.enter_context(tc.psum_pool(name="ps_v", bufs=2))
+        ctx.enter_context(tc.manual_schedule())
+
+        sc_raw = keep.tile([P, DL], U8, align_bytes=64, name="sc_raw")
+        sc_w = keep.tile([P, DL], U8, align_bytes=64, name="sc_w")
+        sc_kv = keep.tile([P, DL], U8, align_bytes=64, name="sc_kv")
+        dummy = keep.tile([P, 1], F32, name="dummy")
+        nc.vector.memset(dummy[:], 1.0)
+        nc.vector.memset(sc_raw[:].bitcast(I32), 0)
+        nc.vector.memset(sc_w[:].bitcast(I32), 0)
+        dummy_out = keep.tile([P, 1], F32, name="dummy_out")
+        nc.scalar.activation(dummy_out[:], dummy[:], ACT.Abs_reciprocal_sqrt)
+        ident = keep.tile([P, P], F32, name="ident")
+        make_identity(nc, ident[:])
+
+        xs_scale = keep.tile([P, 2, 4], F32, name="xs_scale")
+        x_tiles = []
+        for s in range(NLOAD):
+            xt_in = xin.tile([P, RUN, C], U8, align_bytes=64, name="xt_in")
+            x_tiles.append(xt_in)
+        nc.sync.dma_start(out=x_tiles[0][:, 0, :], in_=x_v[0][:, 0, :])
+        nc.sync.dma_start(out=xs_scale[:], in_=x_scale.rearrange("a b (g p t) -> p (a b g) t", p=P, t=4))
+        nc.sync.dma_start(out=x_tiles[0][:, 1:RUN, :], in_=x_v[0][:, 1:RUN, :])
+        kv_raw = keep.tile([P, 2, DL], I32, align_bytes=64, name="kv_raw")
+        nc.sync.dma_start(out=kv_raw[:], in_=w_kv_words.rearrange("g p n t -> p g (n t)").bitcast(I32))
+        kv_s = w_kv_scales.bitcast(I32)
+        for q in range(4):
+            nc.sync.dma_start(out=sc_raw[32 * q : 32 * q + 8, :].bitcast(I32), in_=kv_s[:, 4 * q : 4 * q + 4, :])
+        nc.sync.dma_start(out=x_tiles[1][:], in_=x_v[1])
+        kr_w = keep.tile([P, 2, NKV * DR], I32, align_bytes=64, name="kr_w")
+        nc.sync.dma_start(out=kr_w[:], in_=w_krope_words.rearrange("g p n t -> p g (n t)").bitcast(I32))
+        kr_s = w_krope_scales.bitcast(I32)
+        for q in range(4):
+            nc.sync.dma_start(
+                out=sc_w[32 * q + 8 : 32 * q + 16, 0 : NKV * DR].bitcast(I32), in_=kr_s[:, 4 * q : 4 * q + 4, :]
+            )
+        cs_in = keep.tile([P, 2, NT // 2, DR // 2], BF16, name="cs_in")
+        for j, src in enumerate((cos, sin)):
+            nc.sync.dma_start(
+                out=cs_in[:, j].rearrange("p (s i) c -> p s i c", i=RUN),
+                in_=src.rearrange("(s p i) c -> p s i c", p=P, i=RUN),
+            )
+        ku_w = keep.tile([P, NKV * DN], I32, align_bytes=64, name="ku_w")
+        nc.sync.dma_start(out=ku_w[:], in_=w_kup_words[0].rearrange("p n t -> p (n t)").bitcast(I32))
+        vu_w = keep.tile([P, NKV * HD], I32, align_bytes=64, name="vu_w")
+        nc.sync.dma_start(out=vu_w[:], in_=w_vup_words[0].rearrange("p n t -> p (n t)").bitcast(I32))
+        vu_s = w_vup_scales.bitcast(I32)
+        ku_s = w_kup_scales.bitcast(I32)
+        for q in range(4):
+            nc.sync.dma_start(out=sc_w[32 * q : 32 * q + 4, :].bitcast(I32), in_=vu_s[0, 4 * q : 4 * q + 4, :])
+            nc.sync.dma_start(
+                out=sc_w[32 * q + 4 : 32 * q + 8, 0 : NKV * DN].bitcast(I32), in_=ku_s[0, 4 * q : 4 * q + 4, :]
+            )
+        for s in range(2, NLOAD):
+            nc.sync.dma_start(out=x_tiles[s][:], in_=x_v[s])
+
+        kv_w = keep.tile([P, 2, DL], I32, align_bytes=64, name="kv_w")
+        trig = keep.tile([P, NT // 2, 2, 2, DR // 2], BF16, name="trig")
+
+        def permute_kv():
+            nc.gpsimd.tensor_copy(
+                out=kv_w[:].rearrange("p g (t m) -> p g t m", t=4), in_=kv_raw[:].rearrange("p g (m t) -> p g t m", t=4)
+            )
+            nc.gpsimd.tensor_copy(
+                out=sc_kv[:].rearrange("p (t m) -> p t m", t=4), in_=sc_raw[:].rearrange("p (m t) -> p t m", t=4)
+            )
+
+        def build_trig():
+            nc.scalar.copy(trig[:, :, 0, 0, :], cs_in[:, 0])
+            nc.scalar.copy(trig[:, :, 0, 1, :], cs_in[:, 0])
+            nc.scalar.mul(trig[:, :, 1, 0, :], cs_in[:, 1], -1.0)
+            nc.scalar.copy(trig[:, :, 1, 1, :], cs_in[:, 1])
+
+        live = [{} for n in range(NT)]
+
+        def widen(n):
+            t = live[n]
+            t["xs"] = pools["xs"].tile([P, C], BF16, align_bytes=64, name="xs")
+            xb = x_tiles[n // RUN][:, n % RUN, :].bitcast(FP8)
+            if n < 2:
+                nc.vector.tensor_copy(t["xs"][:, 0:512], xb[:, 0:512])
+                nc.scalar.copy(t["xs"][:, 512:C], xb[:, 512:C])
+            elif n < 5:
+                nc.scalar.copy(t["xs"][:, 0:512], xb[:, 0:512])
+                nc.scalar.copy(t["xs"][:, 512:C], xb[:, 512:C])
+            else:
+                nc.gpsimd.tensor_copy(t["xs"][:], xb)
+
+        def transposes(n):
+            t = live[n]
+            words = t["xs"][:].bitcast(F32)
+            t["xt"] = ps_x.tile([P, 4, P], F32, name="xt")
+            for g in range(2):
+                for u in range(2):
+                    nc.tensor.transpose(
+                        t["xt"][:, 2 * g + u, :], words[:, 256 * g + u : 256 * (g + 1) : 2], ident[:]
+                    )
+
+        def copy_x(n):
+            t = live[n]
+            t["xg"] = pools["xg"].tile([P, 2, P, 4], BF16, align_bytes=64, name="xg")
+            pairs = t["xt"][:].rearrange("p m r -> p (m r)").bitcast(BF16).rearrange("p (g u r e) -> p g u r e", g=2, u=2, e=2)
+            for g in range(2):
+                nc.vector.tensor_tensor(
+                    t["xg"][:, g].rearrange("p r (u e) -> p r u e", e=2),
+                    pairs[:, g].rearrange("p u r e -> p r u e"),
+                    xs_scale[:, g].rearrange("p (u e) -> p u e", e=2).unsqueeze(1).to_broadcast([P, P, 2, 2]),
+                    op=ALU.mult,
+                )
+
+        def quant_x(n):
+            t = live[n]
+            t["xq"] = pools["xq"].tile([P, 2, P], U32, align_bytes=64, name="xq")
+            t["xqs"] = pools["xq"].tile([P, 2, P], U8, align_bytes=64, name="xqs")
+            nc.vector.quantize_mx(
+                out=t["xq"][:].rearrange("p g r -> p (g r)").bitcast(FP8X4),
+                scales=t["xqs"][:].rearrange("p g r -> p (g r)"),
+                in_=t["xg"][:].rearrange("p g r j -> p (g r j)"),
+            )
+
+        def mm_lat(n):
+            t = live[n]
+            t["lat"] = ps_l.tile([P, 4, P], F32, name="lat")
+            for j in range(4):
+                for g in range(2):
+                    nc.tensor.matmul_mx(
+                        out=t["lat"][:, j, :],
+                        lhsT=kv_w[:, g, P * j : P * (j + 1)].bitcast(FP8X4),
+                        lhsT_scale=sc_kv[4 * g : P, P * j : P * (j + 1)],
+                        rhs=t["xq"][:, g, :].bitcast(FP8X4),
+                        rhs_scale=t["xqs"][:, g, :],
+                        start=(g == 0),
+                        stop=(g == 1),
+                    )
+
+        def mm_rope(n):
+            t = live[n]
+            t["rp"] = ps_r.tile([P, NKV, DR], F32, name="rp")
+            for g in range(2):
+                nc.tensor.matmul_mx(
+                    out=t["rp"][:].rearrange("p h d -> p (h d)"),
+                    lhsT=t["xq"][:, g, :].bitcast(FP8X4),
+                    lhsT_scale=t["xqs"][:, g, :],
+                    rhs=kr_w[:, g, :].bitcast(FP8X4),
+                    rhs_scale=sc_w[8 + 4 * g : P, 0 : NKV * DR],
+                    start=(g == 0),
+                    stop=(g == 1),
+                )
+
+        def copy_lat(n):
+            t = live[n]
+            t["lg"] = pools["lg"].tile([P, P, 4], BF16, align_bytes=64, name="lg")
+            if n < 30:
+                nc.scalar.copy(t["lg"][:], t["lat"][:].rearrange("p j r -> p r j"))
+            else:
+                nc.vector.tensor_copy(t["lg"][:], t["lat"][:].rearrange("p j r -> p r j"))
+
+        def quant_lat(n):
+            t = live[n]
+            t["lq"] = pools["lq"].tile([P, P], U32, align_bytes=64, name="lq")
+            t["lqs"] = pools["lq"].tile([P, P], U8, align_bytes=64, name="lqs")
+            nc.vector.quantize_mx(
+                out=t["lq"][:].bitcast(FP8X4), scales=t["lqs"][:], in_=t["lg"][:].rearrange("p r j -> p (r j)")
+            )
+
+        def mm_second(n):
+            t = live[n]
+            t["np"] = ps_n.tile([P, NKV, DN], F32, name="np")
+            nc.tensor.matmul_mx(
+                out=t["np"][:].rearrange("p h d -> p (h d)"),
+                lhsT=t["lq"][:].bitcast(FP8X4),
+                lhsT_scale=t["lqs"][:],
+                rhs=ku_w[:].bitcast(FP8X4),
+                rhs_scale=sc_w[4:P, 0 : NKV * DN],
+                start=True,
+                stop=True,
+            )
+            t["vp"] = ps_v.tile([P, NKV * HD], F32, name="vp")
+            nc.tensor.matmul_mx(
+                out=t["vp"][:],
+                lhsT=t["lq"][:].bitcast(FP8X4),
+                lhsT_scale=t["lqs"][:],
+                rhs=vu_w[:].bitcast(FP8X4),
+                rhs_scale=sc_w[:],
+                start=True,
+                stop=True,
+            )
+
+        def rope_products(n):
+            t = live[n]
+            t["pr"] = pools["pr"].tile([P, NKV, 2, 2, DR // 2], F32, name="pr")
+            shape = [P, NKV, 2, DR]
+            nc.vector.tensor_tensor(
+                t["pr"][:].rearrange("p h a b c -> p h a (b c)"),
+                t["rp"][:].unsqueeze(2).to_broadcast(shape),
+                trig[:, n % (NT // 2)].rearrange("p a b c -> p a (b c)").unsqueeze(1).to_broadcast(shape),
+                op=ALU.mult,
+            )
+
+        def rope_add(n):
+            t = live[n]
+            t["kc"] = pools["kc"].tile([P, NKV, HD], F32, name="kc")
+            add_engine = nc.gpsimd if (n * 8) % 8 < 8 and n < 32 else nc.vector
+            add_engine.tensor_tensor(
+                t["kc"][:, :, 0:DR].rearrange("p h (b c) -> p h b c", b=2),
+                t["pr"][:, :, 0],
+                t["pr"][:, :, 1, ::-1, :],
+                op=ALU.add,
+            )
+
+        def copy_nope(n):
+            t = live[n]
+            if n < 33:
+                nc.scalar.copy(t["kc"][:, :, DR:HD], t["np"][:])
+            else:
+                nc.vector.tensor_copy(t["kc"][:, :, DR:HD], t["np"][:])
+
+        def copy_v(n):
+            t = live[n]
+            t["vo"] = pools["vo"].tile([P, NKV * HD], F32, name="vo")
+            if n < 30:
+                nc.scalar.copy(t["vo"][:], t["vp"][:])
+            else:
+                nc.vector.tensor_copy(t["vo"][:], t["vp"][:])
+            nc.sync.dma_start(out=v_v[n // RUN, n % RUN], in_=t["vo"][:])
+
+        def squares(n):
+            t = live[n]
+            t["ss"] = pools["ss"].tile([P, NKV], F32, name="ss")
+            for h in range(NKV):
+                junk = pools["junk"].tile([P, HD], F32, name="junk")
+                nc.scalar.activation(junk[:], t["kc"][:, h, :], ACT.Square, accum_out=t["ss"][:, h : h + 1])
+
+        def rsq(n):
+            t = live[n]
+            t["rs"] = pools["ss"].tile([P, NKV], F32, name="rs")
+            nc.scalar.activation(t["rs"][:], t["ss"][:], ACT.Abs_reciprocal_sqrt, bias=EPS, scale=1.0 / HD)
+
+        def scale_k(n):
+            t = live[n]
+            t["ko"] = pools["ko"].tile([P, NKV, HD], F32, name="ko")
+            if n < 21:
+                heads_v = 1 + (1 if n % 4 < 1 else 0)
+            else:
+                heads_v = 4
+            for h in range(NKV):
+                if h < heads_v:
+                    nc.vector.tensor_scalar(
+                        out=t["ko"][:, h, :], in0=t["kc"][:, h, :], scalar1=t["rs"][:, h : h + 1], scalar2=None, op0=ALU.mult
+                    )
+                else:
+                    nc.scalar.activation(t["ko"][:, h, :], t["kc"][:, h, :], ACT.Copy, scale=t["rs"][:, h : h + 1])
+            nc.sync.dma_start(out=k_v[n // RUN, n % RUN], in_=t["ko"][:].rearrange("p h d -> p (h d)"))
+            live[n] = None
+
+        order = [
+            (scale_k, 12),
+            (copy_v, 10),
+            (copy_lat, 8),
+            (mm_rope, 8),
+            (squares, 10),
+            (mm_second, 9),
+            (copy_x, 4),
+            (rope_products, 8),
+            (mm_lat, 7),
+            (transposes, 3),
+            (widen, 2),
+            (copy_nope, 9),
+            (quant_lat, 8),
+            (quant_x, 6),
+            (rope_add, 8),
+            (rsq, 10),
+        ]
+        for n in range(2, NT + 12):
+            if n == 7:
+                permute_kv()
+            if n == 8:
+                build_trig()
+            for stage, lag in order:
+                if 0 <= n - lag < NT:
+                    stage(n - lag)

@@ -18,12 +18,15 @@ FP8 = mybir.dt.float8_e4m3fn
 FP8X4 = mybir.dt.float8_e4m3fn_x4
 ACT = mybir.ActivationFunctionType
 ALU = mybir.AluOpType
+AXIS = mybir.AxisListType
 
 P = 128
 RUN = 4
 NT = TOK // P
 NLOAD = NT // RUN
-BUFS = dict(xs=6, xg=4, xq=6, lg=4, lq=4, pr=4, kc=6, ko=4, vo=4, ss=6, junk=6)
+PAIR = 2
+NU = NT // PAIR
+NH = PAIR * NKV
 
 
 def tile_mlacausalselfattention_pa_t_w8_kernel(
@@ -32,65 +35,61 @@ def tile_mlacausalselfattention_pa_t_w8_kernel(
 ):
     nc = tc.nc
     x_v = x_bytes.rearrange("b t k -> (b t) k").rearrange("(s p i) k -> s p i k", p=P, i=RUN)
-    k_v = out_k.rearrange("b t h d -> (b t) (h d)").rearrange("(s p i) c -> s i p c", p=P, i=RUN)
-    v_v = out_v.rearrange("b t h d -> (b t) (h d)").rearrange("(s p i) c -> s i p c", p=P, i=RUN)
+    k_v = out_k.rearrange("b t h d -> (b t) (h d)").rearrange("(s p i) c -> s p i c", p=P, i=RUN)
+    v_v = out_v.rearrange("b t h d -> (b t) (h d)").rearrange("(s p i) c -> s p i c", p=P, i=RUN)
 
     with ExitStack() as ctx:
         keep = ctx.enter_context(tc.tile_pool(name="keep", bufs=1))
-        xin = ctx.enter_context(tc.tile_pool(name="xin", bufs=NLOAD))
-        pools = {}
-        for name, bufs in BUFS.items():
-            pools[name] = ctx.enter_context(tc.tile_pool(name=name, bufs=bufs))
-        ps_x = ctx.enter_context(tc.psum_pool(name="ps_x", bufs=2))
-        ps_l = ctx.enter_context(tc.psum_pool(name="ps_l", bufs=2))
-        ps_r = ctx.enter_context(tc.psum_pool(name="ps_r", bufs=1))
-        ps_n = ctx.enter_context(tc.psum_pool(name="ps_n", bufs=1))
-        ps_v = ctx.enter_context(tc.psum_pool(name="ps_v", bufs=2))
+        two = ctx.enter_context(tc.tile_pool(name="two", bufs=2))
+        three = ctx.enter_context(tc.tile_pool(name="three", bufs=3))
+        ps_one = ctx.enter_context(tc.psum_pool(name="ps_one", bufs=1))
+        ps_two = ctx.enter_context(tc.psum_pool(name="ps_two", bufs=2))
+        ps_three = ctx.enter_context(tc.psum_pool(name="ps_three", bufs=3))
         ctx.enter_context(tc.manual_schedule())
 
         sc_raw = keep.tile([P, DL], U8, align_bytes=64, name="sc_raw")
         sc_w = keep.tile([P, DL], U8, align_bytes=64, name="sc_w")
         sc_kv = keep.tile([P, DL], U8, align_bytes=64, name="sc_kv")
-        dummy = keep.tile([P, 1], F32, name="dummy")
-        nc.vector.memset(dummy[:], 1.0)
+        sc_kr = keep.tile([P, NKV * DR], U8, align_bytes=64, name="sc_kr")
         nc.vector.memset(sc_raw[:].bitcast(I32), 0)
+        nc.vector.memset(sc_kr[:].bitcast(I32), 0)
         nc.vector.memset(sc_w[:].bitcast(I32), 0)
-        dummy_out = keep.tile([P, 1], F32, name="dummy_out")
-        nc.scalar.activation(dummy_out[:], dummy[:], ACT.Abs_reciprocal_sqrt)
         ident = keep.tile([P, P], F32, name="ident")
         make_identity(nc, ident[:])
 
+        x_rows = {}
+
+        def load_x(s, i0, i1):
+            xin = keep.tile([P, i1 - i0, C], U8, align_bytes=64, name="xin%d_%d" % (s, i0))
+            nc.sync.dma_start(out=xin[:], in_=x_v[s][:, i0:i1, :])
+            for i in range(i0, i1):
+                x_rows[RUN * s + i] = (xin, i - i0)
+
+        load_x(0, 0, 1)
         xs_scale = keep.tile([P, 2, 4], F32, name="xs_scale")
-        x_tiles = []
-        for s in range(NLOAD):
-            xt_in = xin.tile([P, RUN, C], U8, align_bytes=64, name="xt_in")
-            x_tiles.append(xt_in)
-        nc.sync.dma_start(out=x_tiles[0][:, 0, :], in_=x_v[0][:, 0, :])
         nc.sync.dma_start(out=xs_scale[:], in_=x_scale.rearrange("a b (g p t) -> p (a b g) t", p=P, t=4))
-        nc.sync.dma_start(out=x_tiles[0][:, 1:RUN, :], in_=x_v[0][:, 1:RUN, :])
+        load_x(0, 1, RUN)
         kv_raw = keep.tile([P, 2, DL], I32, align_bytes=64, name="kv_raw")
         nc.sync.dma_start(out=kv_raw[:], in_=w_kv_words.rearrange("g p n t -> p g (n t)").bitcast(I32))
         kv_s = w_kv_scales.bitcast(I32)
         for q in range(4):
             nc.sync.dma_start(out=sc_raw[32 * q : 32 * q + 8, :].bitcast(I32), in_=kv_s[:, 4 * q : 4 * q + 4, :])
-        nc.sync.dma_start(out=x_tiles[1][:], in_=x_v[1])
+        load_x(1, 0, 4)
         kr_w = keep.tile([P, 2, NKV * DR], I32, align_bytes=64, name="kr_w")
         nc.sync.dma_start(out=kr_w[:], in_=w_krope_words.rearrange("g p n t -> p g (n t)").bitcast(I32))
         kr_s = w_krope_scales.bitcast(I32)
         for q in range(4):
-            nc.sync.dma_start(
-                out=sc_w[32 * q + 8 : 32 * q + 16, 0 : NKV * DR].bitcast(I32), in_=kr_s[:, 4 * q : 4 * q + 4, :]
-            )
+            nc.sync.dma_start(out=sc_kr[32 * q : 32 * q + 8, :].bitcast(I32), in_=kr_s[:, 4 * q : 4 * q + 4, :])
         cs_in = keep.tile([P, 2, NT // 2, DR // 2], BF16, name="cs_in")
         for j, src in enumerate((cos, sin)):
             nc.sync.dma_start(
                 out=cs_in[:, j].rearrange("p (s i) c -> p s i c", i=RUN),
                 in_=src.rearrange("(s p i) c -> p s i c", p=P, i=RUN),
             )
-        ku_w = keep.tile([P, NKV * DN], I32, align_bytes=64, name="ku_w")
-        nc.sync.dma_start(out=ku_w[:], in_=w_kup_words[0].rearrange("p n t -> p (n t)").bitcast(I32))
         vu_w = keep.tile([P, NKV * HD], I32, align_bytes=64, name="vu_w")
         nc.sync.dma_start(out=vu_w[:], in_=w_vup_words[0].rearrange("p n t -> p (n t)").bitcast(I32))
+        ku_w = keep.tile([P, NKV * DN], I32, align_bytes=64, name="ku_w")
+        nc.sync.dma_start(out=ku_w[:], in_=w_kup_words[0].rearrange("p n t -> p (n t)").bitcast(I32))
         vu_s = w_vup_scales.bitcast(I32)
         ku_s = w_kup_scales.bitcast(I32)
         for q in range(4):
@@ -99,7 +98,7 @@ def tile_mlacausalselfattention_pa_t_w8_kernel(
                 out=sc_w[32 * q + 4 : 32 * q + 8, 0 : NKV * DN].bitcast(I32), in_=ku_s[0, 4 * q : 4 * q + 4, :]
             )
         for s in range(2, NLOAD):
-            nc.sync.dma_start(out=x_tiles[s][:], in_=x_v[s])
+            load_x(s, 0, RUN)
 
         kv_w = keep.tile([P, 2, DL], I32, align_bytes=64, name="kv_w")
         trig = keep.tile([P, NT // 2, 2, 2, DR // 2], BF16, name="trig")
@@ -112,217 +111,281 @@ def tile_mlacausalselfattention_pa_t_w8_kernel(
                 out=sc_kv[:].rearrange("p (t m) -> p t m", t=4), in_=sc_raw[:].rearrange("p (m t) -> p t m", t=4)
             )
 
-        def build_trig():
-            nc.scalar.copy(trig[:, :, 0, 0, :], cs_in[:, 0])
-            nc.scalar.copy(trig[:, :, 0, 1, :], cs_in[:, 0])
-            nc.scalar.mul(trig[:, :, 1, 0, :], cs_in[:, 1], -1.0)
-            nc.scalar.copy(trig[:, :, 1, 1, :], cs_in[:, 1])
+        def build_trig(n0, n1):
+            nc.scalar.copy(trig[:, n0:n1, 0, 0, :], cs_in[:, 0, n0:n1])
+            nc.scalar.copy(trig[:, n0:n1, 0, 1, :], cs_in[:, 0, n0:n1])
+            nc.scalar.mul(trig[:, n0:n1, 1, 0, :], cs_in[:, 1, n0:n1], -1.0)
+            nc.scalar.copy(trig[:, n0:n1, 1, 1, :], cs_in[:, 1, n0:n1])
 
-        live = [{} for n in range(NT)]
+        live = [{} for u in range(NU)]
 
-        def widen(n):
-            t = live[n]
-            t["xs"] = pools["xs"].tile([P, C], BF16, align_bytes=64, name="xs")
-            xb = x_tiles[n // RUN][:, n % RUN, :].bitcast(FP8)
-            if n < 2:
-                nc.vector.tensor_copy(t["xs"][:, 0:512], xb[:, 0:512])
-                nc.scalar.copy(t["xs"][:, 512:C], xb[:, 512:C])
-            elif n < 5:
-                nc.scalar.copy(t["xs"][:, 0:512], xb[:, 0:512])
-                nc.scalar.copy(t["xs"][:, 512:C], xb[:, 512:C])
-            else:
-                nc.gpsimd.tensor_copy(t["xs"][:], xb)
+        def x_fp8(n, count):
+            xin, row = x_rows[n]
+            return xin[:, row : row + count, :].rearrange("p i k -> p (i k)").bitcast(FP8)
 
-        def transposes(n):
-            t = live[n]
-            words = t["xs"][:].bitcast(F32)
-            t["xt"] = ps_x.tile([P, 4, P], F32, name="xt")
+        def new_xs(u):
+            live[u]["xs"] = keep.tile([P, PAIR * C], BF16, align_bytes=64, name="xslot%d" % (u % 3))
+
+        def widen(u):
+            t = live[u]
+            new_xs(u)
+            nc.gpsimd.tensor_copy(t["xs"][:], x_fp8(PAIR * u, PAIR))
+
+        def transposes(u, i):
+            t = live[u]
+            words = t["xs"][:, C * i : C * (i + 1)].bitcast(F32)
+            t["xt", i] = ps_two.tile([P, 4, P], F32, name="xt")
             for g in range(2):
-                for u in range(2):
-                    nc.tensor.transpose(
-                        t["xt"][:, 2 * g + u, :], words[:, 256 * g + u : 256 * (g + 1) : 2], ident[:]
-                    )
+                for w in range(2):
+                    nc.tensor.transpose(t["xt", i][:, 2 * g + w, :], words[:, 256 * g + w : 256 * (g + 1) : 2], ident[:])
 
-        def copy_x(n):
-            t = live[n]
-            t["xg"] = pools["xg"].tile([P, 2, P, 4], BF16, align_bytes=64, name="xg")
-            pairs = t["xt"][:].rearrange("p m r -> p (m r)").bitcast(BF16).rearrange("p (g u r e) -> p g u r e", g=2, u=2, e=2)
+        def copy_x(u, i):
+            t = live[u]
+            if i == 0:
+                t["xg"] = keep.tile([P, PAIR, 2, P, 4], BF16, align_bytes=64, name="xslot%d" % (u % 3))
+            pairs = t["xt", i][:].rearrange("p m r -> p (m r)").bitcast(BF16).rearrange("p (g w r e) -> p g r w e", g=2, w=2, e=2)
             for g in range(2):
                 nc.vector.tensor_tensor(
-                    t["xg"][:, g].rearrange("p r (u e) -> p r u e", e=2),
-                    pairs[:, g].rearrange("p u r e -> p r u e"),
-                    xs_scale[:, g].rearrange("p (u e) -> p u e", e=2).unsqueeze(1).to_broadcast([P, P, 2, 2]),
+                    t["xg"][:, i, g].rearrange("p r (w e) -> p r w e", e=2),
+                    pairs[:, g],
+                    xs_scale[:, g].rearrange("p (w e) -> p w e", e=2).unsqueeze(1).to_broadcast([P, P, 2, 2]),
                     op=ALU.mult,
                 )
 
-        def quant_x(n):
-            t = live[n]
-            t["xq"] = pools["xq"].tile([P, 2, P], U32, align_bytes=64, name="xq")
-            t["xqs"] = pools["xq"].tile([P, 2, P], U8, align_bytes=64, name="xqs")
+        def quant_x(u):
+            t = live[u]
+            t["xq"] = two.tile([P, PAIR, 2, P], U32, align_bytes=64, name="xq")
+            t["xqs"] = two.tile([P, PAIR, 2, P], U8, align_bytes=64, name="xqs")
             nc.vector.quantize_mx(
-                out=t["xq"][:].rearrange("p g r -> p (g r)").bitcast(FP8X4),
-                scales=t["xqs"][:].rearrange("p g r -> p (g r)"),
-                in_=t["xg"][:].rearrange("p g r j -> p (g r j)"),
+                out=t["xq"][:].rearrange("p i g r -> p (i g r)").bitcast(FP8X4),
+                scales=t["xqs"][:].rearrange("p i g r -> p (i g r)"),
+                in_=t["xg"][:].rearrange("p i g r j -> p (i g r j)"),
             )
 
-        def mm_lat(n):
-            t = live[n]
-            t["lat"] = ps_l.tile([P, 4, P], F32, name="lat")
+        def mm_lat(u, i):
+            t = live[u]
+            t["lat", i] = ps_three.tile([P, 4, P], F32, name="acc")
             for j in range(4):
                 for g in range(2):
                     nc.tensor.matmul_mx(
-                        out=t["lat"][:, j, :],
+                        out=t["lat", i][:, j, :],
                         lhsT=kv_w[:, g, P * j : P * (j + 1)].bitcast(FP8X4),
                         lhsT_scale=sc_kv[4 * g : P, P * j : P * (j + 1)],
-                        rhs=t["xq"][:, g, :].bitcast(FP8X4),
-                        rhs_scale=t["xqs"][:, g, :],
+                        rhs=t["xq"][:, i, g, :].bitcast(FP8X4),
+                        rhs_scale=t["xqs"][:, i, g, :],
                         start=(g == 0),
                         stop=(g == 1),
                     )
 
-        def mm_rope(n):
-            t = live[n]
-            t["rp"] = ps_r.tile([P, NKV, DR], F32, name="rp")
-            for g in range(2):
+        def mm_rope(u):
+            t = live[u]
+            t["rp"] = ps_one.tile([P, PAIR, NKV * DR], F32, name="rp")
+            for i in range(PAIR):
+                for g in range(2):
+                    nc.tensor.matmul_mx(
+                        out=t["rp"][:, i, :],
+                        lhsT=t["xq"][:, i, g, :].bitcast(FP8X4),
+                        lhsT_scale=t["xqs"][:, i, g, :],
+                        rhs=kr_w[:, g, :].bitcast(FP8X4),
+                        rhs_scale=sc_kr[4 * g : P, :],
+                        start=(g == 0),
+                        stop=(g == 1),
+                    )
+
+        def copy_lat(u, i, copy=nc.scalar.copy):
+            t = live[u]
+            if i == 0:
+                t["lg"] = two.tile([P, PAIR, P, 4], BF16, align_bytes=64, name="lg")
+            copy(t["lg"][:, i], t["lat", i][:].rearrange("p j r -> p r j"))
+
+        def quant_lat(u):
+            t = live[u]
+            t["lq"] = two.tile([P, PAIR, P], U32, align_bytes=64, name="lq")
+            t["lqs"] = two.tile([P, PAIR, P], U8, align_bytes=64, name="lqs")
+            nc.vector.quantize_mx(
+                out=t["lq"][:].rearrange("p i r -> p (i r)").bitcast(FP8X4),
+                scales=t["lqs"][:].rearrange("p i r -> p (i r)"),
+                in_=t["lg"][:].rearrange("p i r j -> p (i r j)"),
+            )
+
+        def mm_v(u, i):
+            t = live[u]
+            t["vp", i] = ps_three.tile([P, NKV * HD], F32, name="acc")
+            nc.tensor.matmul_mx(
+                out=t["vp", i][:], lhsT=t["lq"][:, i, :].bitcast(FP8X4), lhsT_scale=t["lqs"][:, i, :],
+                rhs=vu_w[:].bitcast(FP8X4), rhs_scale=sc_w[:], start=True, stop=True,
+            )
+
+        def mm_nope(u):
+            t = live[u]
+            t["np"] = ps_two.tile([P, PAIR, NKV * DN], F32, name="np")
+            for i in range(PAIR):
                 nc.tensor.matmul_mx(
-                    out=t["rp"][:].rearrange("p h d -> p (h d)"),
-                    lhsT=t["xq"][:, g, :].bitcast(FP8X4),
-                    lhsT_scale=t["xqs"][:, g, :],
-                    rhs=kr_w[:, g, :].bitcast(FP8X4),
-                    rhs_scale=sc_w[8 + 4 * g : P, 0 : NKV * DR],
-                    start=(g == 0),
-                    stop=(g == 1),
+                    out=t["np"][:, i, :], lhsT=t["lq"][:, i, :].bitcast(FP8X4), lhsT_scale=t["lqs"][:, i, :],
+                    rhs=ku_w[:].bitcast(FP8X4), rhs_scale=sc_w[4:P, 0 : NKV * DN], start=True, stop=True,
                 )
 
-        def copy_lat(n):
-            t = live[n]
-            t["lg"] = pools["lg"].tile([P, P, 4], BF16, align_bytes=64, name="lg")
-            if n < 30:
-                nc.scalar.copy(t["lg"][:], t["lat"][:].rearrange("p j r -> p r j"))
-            else:
-                nc.vector.tensor_copy(t["lg"][:], t["lat"][:].rearrange("p j r -> p r j"))
-
-        def quant_lat(n):
-            t = live[n]
-            t["lq"] = pools["lq"].tile([P, P], U32, align_bytes=64, name="lq")
-            t["lqs"] = pools["lq"].tile([P, P], U8, align_bytes=64, name="lqs")
-            nc.vector.quantize_mx(
-                out=t["lq"][:].bitcast(FP8X4), scales=t["lqs"][:], in_=t["lg"][:].rearrange("p r j -> p (r j)")
-            )
-
-        def mm_second(n):
-            t = live[n]
-            t["np"] = ps_n.tile([P, NKV, DN], F32, name="np")
-            nc.tensor.matmul_mx(
-                out=t["np"][:].rearrange("p h d -> p (h d)"),
-                lhsT=t["lq"][:].bitcast(FP8X4),
-                lhsT_scale=t["lqs"][:],
-                rhs=ku_w[:].bitcast(FP8X4),
-                rhs_scale=sc_w[4:P, 0 : NKV * DN],
-                start=True,
-                stop=True,
-            )
-            t["vp"] = ps_v.tile([P, NKV * HD], F32, name="vp")
-            nc.tensor.matmul_mx(
-                out=t["vp"][:],
-                lhsT=t["lq"][:].bitcast(FP8X4),
-                lhsT_scale=t["lqs"][:],
-                rhs=vu_w[:].bitcast(FP8X4),
-                rhs_scale=sc_w[:],
-                start=True,
-                stop=True,
-            )
-
-        def rope_products(n):
-            t = live[n]
-            t["pr"] = pools["pr"].tile([P, NKV, 2, 2, DR // 2], F32, name="pr")
-            shape = [P, NKV, 2, DR]
+        def rope_products(u):
+            t = live[u]
+            t["pr"] = two.tile([P, PAIR, NKV, 2, DR], F32, name="pr")
+            shape = [P, PAIR, NKV, 2, DR]
+            n0 = (PAIR * u) % (NT // 2)
             nc.vector.tensor_tensor(
-                t["pr"][:].rearrange("p h a b c -> p h a (b c)"),
-                t["rp"][:].unsqueeze(2).to_broadcast(shape),
-                trig[:, n % (NT // 2)].rearrange("p a b c -> p a (b c)").unsqueeze(1).to_broadcast(shape),
+                t["pr"][:],
+                t["rp"][:].rearrange("p i (h d) -> p i h d", h=NKV).unsqueeze(3).to_broadcast(shape),
+                trig[:, n0 : n0 + PAIR].rearrange("p i a b c -> p i a (b c)").unsqueeze(2).to_broadcast(shape),
                 op=ALU.mult,
             )
 
-        def rope_add(n):
-            t = live[n]
-            t["kc"] = pools["kc"].tile([P, NKV, HD], F32, name="kc")
-            add_engine = nc.gpsimd if (n * 8) % 8 < 8 and n < 32 else nc.vector
-            add_engine.tensor_tensor(
-                t["kc"][:, :, 0:DR].rearrange("p h (b c) -> p h b c", b=2),
-                t["pr"][:, :, 0],
-                t["pr"][:, :, 1, ::-1, :],
-                op=ALU.add,
+        def rope_add(u):
+            t = live[u]
+            t["kr"] = two.tile([P, NH, DR], F32, name="kr")
+            pr = t["pr"][:].rearrange("p i h a (b c) -> p (i h) a b c", b=2)
+            nc.gpsimd.tensor_tensor(
+                t["kr"][:].rearrange("p j (b c) -> p j b c", b=2), pr[:, :, 0], pr[:, :, 1, ::-1, :], op=ALU.add
             )
 
-        def copy_nope(n):
-            t = live[n]
-            if n < 33:
-                nc.scalar.copy(t["kc"][:, :, DR:HD], t["np"][:])
+        def copy_v(u, i, copy=nc.scalar.copy):
+            t = live[u]
+            if i == 0:
+                t["vo"] = two.tile([P, PAIR, NKV * HD], F32, name="vo")
+            copy(t["vo"][:, i, :], t["vp", i][:])
+            if i == PAIR - 1:
+                i0 = (PAIR * u) % RUN
+                nc.sync.dma_start(out=v_v[PAIR * u // RUN][:, i0 : i0 + PAIR, :], in_=t["vo"][:])
+
+        def squares(u, part):
+            t = live[u]
+            if "ss" not in t:
+                t["ss"] = two.tile([P, NH, 2], F32, name="ss")
+            if part == 0:
+                src = t["kr"][:]
             else:
-                nc.vector.tensor_copy(t["kc"][:, :, DR:HD], t["np"][:])
+                src = t["np"][:].rearrange("p i (h d) -> p (i h) d", h=NKV)
+            sq = two.tile([P, NH, DR], F32, name="sq")
+            for j in range(NH):
+                nc.scalar.activation(sq[:, j, :], src[:, j, :], ACT.Square, accum_out=t["ss"][:, j, part : part + 1])
 
-        def copy_v(n):
-            t = live[n]
-            t["vo"] = pools["vo"].tile([P, NKV * HD], F32, name="vo")
-            if n < 30:
-                nc.scalar.copy(t["vo"][:], t["vp"][:])
-            else:
-                nc.vector.tensor_copy(t["vo"][:], t["vp"][:])
-            nc.sync.dma_start(out=v_v[n // RUN, n % RUN], in_=t["vo"][:])
+        def sum_halves(u):
+            t = live[u]
+            t["st"] = two.tile([P, NH], F32, name="st")
+            nc.vector.tensor_reduce(t["st"][:], t["ss"][:], axis=AXIS.X, op=ALU.add)
 
-        def squares(n):
-            t = live[n]
-            t["ss"] = pools["ss"].tile([P, NKV], F32, name="ss")
-            for h in range(NKV):
-                junk = pools["junk"].tile([P, HD], F32, name="junk")
-                nc.scalar.activation(junk[:], t["kc"][:, h, :], ACT.Square, accum_out=t["ss"][:, h : h + 1])
+        def inv_root(u):
+            t = live[u]
+            t["rs"] = two.tile([P, NH], F32, name="rs")
+            nc.scalar.activation(t["rs"][:], t["st"][:], ACT.Abs_reciprocal_sqrt, bias=EPS, scale=1.0 / HD)
 
-        def rsq(n):
-            t = live[n]
-            t["rs"] = pools["ss"].tile([P, NKV], F32, name="rs")
-            nc.scalar.activation(t["rs"][:], t["ss"][:], ACT.Abs_reciprocal_sqrt, bias=EPS, scale=1.0 / HD)
+        def scale_rope(u):
+            t = live[u]
+            t["ko"] = two.tile([P, NH, HD], F32, name="ko")
+            for j in range(NH):
+                nc.scalar.activation(t["ko"][:, j, 0:DR], t["kr"][:, j, :], ACT.Copy, scale=t["rs"][:, j : j + 1])
 
-        def scale_k(n):
-            t = live[n]
-            t["ko"] = pools["ko"].tile([P, NKV, HD], F32, name="ko")
-            if n < 21:
-                heads_v = 1 + (1 if n % 4 < 1 else 0)
-            else:
-                heads_v = 4
-            for h in range(NKV):
-                if h < heads_v:
-                    nc.vector.tensor_scalar(
-                        out=t["ko"][:, h, :], in0=t["kc"][:, h, :], scalar1=t["rs"][:, h : h + 1], scalar2=None, op0=ALU.mult
-                    )
-                else:
-                    nc.scalar.activation(t["ko"][:, h, :], t["kc"][:, h, :], ACT.Copy, scale=t["rs"][:, h : h + 1])
-            nc.sync.dma_start(out=k_v[n // RUN, n % RUN], in_=t["ko"][:].rearrange("p h d -> p (h d)"))
-            live[n] = None
+        def scale_rope_vector(u):
+            t = live[u]
+            t["ko"] = two.tile([P, NH, HD], F32, name="ko")
+            for j in range(NH):
+                nc.vector.tensor_scalar(
+                    out=t["ko"][:, j, 0:DR], in0=t["kr"][:, j, :], scalar1=t["rs"][:, j : j + 1], scalar2=None, op0=ALU.mult
+                )
 
-        order = [
-            (scale_k, 12),
-            (copy_v, 10),
-            (copy_lat, 8),
-            (mm_rope, 8),
-            (squares, 10),
-            (mm_second, 9),
-            (copy_x, 4),
-            (rope_products, 8),
-            (mm_lat, 7),
-            (transposes, 3),
-            (widen, 2),
-            (copy_nope, 9),
-            (quant_lat, 8),
-            (quant_x, 6),
-            (rope_add, 8),
-            (rsq, 10),
-        ]
-        for n in range(2, NT + 12):
-            if n == 7:
-                permute_kv()
-            if n == 8:
-                build_trig()
-            for stage, lag in order:
-                if 0 <= n - lag < NT:
-                    stage(n - lag)
+        def scale_nope(u):
+            t = live[u]
+            nc.vector.tensor_tensor(
+                t["ko"][:, :, DR:HD],
+                t["np"][:].rearrange("p i (h d) -> p (i h) d", h=NKV),
+                t["rs"][:].unsqueeze(2).to_broadcast([P, NH, DN]),
+                op=ALU.mult,
+            )
+            i0 = (PAIR * u) % RUN
+            nc.sync.dma_start(
+                out=k_v[PAIR * u // RUN][:, i0 : i0 + PAIR, :], in_=t["ko"][:].rearrange("p (i h) d -> p i (h d)", i=PAIR)
+            )
+
+        def run(stage, u, *rest):
+            if 0 <= u < NU:
+                stage(u, *rest)
+
+        for u in range(3):
+            live[u]["xs"] = keep.tile([P, PAIR * C], BF16, align_bytes=64, name="xs_head%d" % u)
+        for n in range(PAIR):
+            nc.vector.tensor_copy(live[0]["xs"][:, C * n : C * n + C // 2], x_fp8(n, 1)[:, 0 : C // 2])
+            nc.scalar.copy(live[0]["xs"][:, C * n + C // 2 : C * (n + 1)], x_fp8(n, 1)[:, C // 2 : C])
+        for n in range(PAIR, 3 * PAIR):
+            nc.scalar.copy(live[n // PAIR]["xs"][:, C * (n % PAIR) : C * (n % PAIR + 1)], x_fp8(n, 1))
+        permute_kv()
+        build_trig(0, RUN)
+        transposes(0, 0)
+        transposes(0, 1)
+
+        for u in range(-1, NU - 1):
+            run(quant_x, u)
+            run(quant_lat, u - 1)
+            if u >= 0:
+                run(widen, u + 3)
+            run(rope_add, u - 1)
+            run(copy_v, u - 2, 0)
+            run(copy_v, u - 2, 1)
+            run(mm_rope, u)
+            run(mm_lat, u, 0)
+            run(mm_lat, u, 1)
+            run(squares, u - 2, 0)
+            run(squares, u - 2, 1)
+            run(copy_x, u + 1, 0)
+            run(transposes, u + 2, 0)
+            run(copy_x, u + 1, 1)
+            run(sum_halves, u - 2)
+            run(copy_lat, u, 0)
+            run(inv_root, u - 2)
+            run(copy_lat, u, 1)
+            run(scale_rope, u - 2)
+            if u == 0:
+                build_trig(RUN, NT // 2)
+            run(mm_v, u - 1, 0)
+            run(mm_v, u - 1, 1)
+            run(mm_nope, u - 1)
+            run(rope_products, u)
+            run(transposes, u + 2, 1)
+            run(scale_nope, u - 2)
+        quant_x(NU - 1)
+        quant_lat(NU - 2)
+        rope_add(NU - 2)
+        copy_v(NU - 3, 0)
+        copy_v(NU - 3, 1)
+        mm_lat(NU - 1, 0)
+        mm_lat(NU - 1, 1)
+        mm_rope(NU - 1)
+        squares(NU - 3, 0)
+        squares(NU - 3, 1)
+        mm_v(NU - 2, 0)
+        copy_lat(NU - 1, 0, nc.vector.tensor_copy)
+        mm_nope(NU - 2)
+        copy_lat(NU - 1, 1, nc.vector.tensor_copy)
+        mm_v(NU - 2, 1)
+        sum_halves(NU - 3)
+        rope_products(NU - 1)
+        inv_root(NU - 3)
+        squares(NU - 2, 0)
+        quant_lat(NU - 1)
+        rope_add(NU - 1)
+        scale_rope_vector(NU - 3)
+        scale_nope(NU - 3)
+        squares(NU - 2, 1)
+        mm_nope(NU - 1)
+        copy_v(NU - 2, 0, nc.vector.tensor_copy)
+        mm_v(NU - 1, 0)
+        sum_halves(NU - 2)
+        copy_v(NU - 2, 1, nc.vector.tensor_copy)
+        inv_root(NU - 2)
+        mm_v(NU - 1, 1)
+        squares(NU - 1, 1)
+        squares(NU - 1, 0)
+        scale_rope_vector(NU - 2)
+        scale_nope(NU - 2)
+        copy_v(NU - 1, 0, nc.vector.tensor_copy)
+        sum_halves(NU - 1)
+        inv_root(NU - 1)
+        copy_v(NU - 1, 1)
+        scale_rope_vector(NU - 1)
+        scale_nope(NU - 1)

@@ -1,3 +1,4 @@
+import math
 from contextlib import ExitStack
 
 import concourse.mybir as mybir
@@ -27,6 +28,8 @@ NLOAD = NT // RUN
 PAIR = 2
 NU = NT // PAIR
 NH = PAIR * NKV
+STAT_PAIRS = 1
+HEADS_V = 3
 
 
 def tile_mlacausalselfattention_pa_t_w8_kernel(
@@ -44,7 +47,7 @@ def tile_mlacausalselfattention_pa_t_w8_kernel(
         three = ctx.enter_context(tc.tile_pool(name="three", bufs=3))
         ps_one = ctx.enter_context(tc.psum_pool(name="ps_one", bufs=1))
         ps_two = ctx.enter_context(tc.psum_pool(name="ps_two", bufs=2))
-        ps_three = ctx.enter_context(tc.psum_pool(name="ps_three", bufs=3))
+        ps_three = ctx.enter_context(tc.psum_pool(name="ps_three", bufs=4))
         ctx.enter_context(tc.manual_schedule())
 
         sc_raw = keep.tile([P, DL], U8, align_bytes=64, name="sc_raw")
@@ -124,7 +127,7 @@ def tile_mlacausalselfattention_pa_t_w8_kernel(
             return xin[:, row : row + count, :].rearrange("p i k -> p (i k)").bitcast(FP8)
 
         def new_xs(u):
-            live[u]["xs"] = keep.tile([P, PAIR * C], BF16, align_bytes=64, name="xslot%d" % (u % 3))
+            live[u]["xs"] = three.tile([P, PAIR * C], BF16, align_bytes=64, name="xs")
 
         def widen(u):
             t = live[u]
@@ -139,12 +142,12 @@ def tile_mlacausalselfattention_pa_t_w8_kernel(
                 for w in range(2):
                     nc.tensor.transpose(t["xt", i][:, 2 * g + w, :], words[:, 256 * g + w : 256 * (g + 1) : 2], ident[:])
 
-        def copy_x(u, i):
+        def copy_x(u, i, passes=(0, 1)):
             t = live[u]
-            if i == 0:
-                t["xg"] = keep.tile([P, PAIR, 2, P, 4], BF16, align_bytes=64, name="xslot%d" % (u % 3))
+            if "xg" not in t:
+                t["xg"] = two.tile([P, PAIR, 2, P, 4], BF16, align_bytes=64, name="xg")
             pairs = t["xt", i][:].rearrange("p m r -> p (m r)").bitcast(BF16).rearrange("p (g w r e) -> p g r w e", g=2, w=2, e=2)
-            for g in range(2):
+            for g in passes:
                 nc.vector.tensor_tensor(
                     t["xg"][:, i, g].rearrange("p r (w e) -> p r w e", e=2),
                     pairs[:, g],
@@ -195,7 +198,7 @@ def tile_mlacausalselfattention_pa_t_w8_kernel(
         def copy_lat(u, i, copy=nc.scalar.copy):
             t = live[u]
             if i == 0:
-                t["lg"] = two.tile([P, PAIR, P, 4], BF16, align_bytes=64, name="lg")
+                t["lg"] = keep.tile([P, PAIR, P, 4], BF16, align_bytes=64, name="lk%d" % (u % 3))
             copy(t["lg"][:, i], t["lat", i][:].rearrange("p j r -> p r j"))
 
         def quant_lat(u):
@@ -218,7 +221,7 @@ def tile_mlacausalselfattention_pa_t_w8_kernel(
 
         def mm_nope(u):
             t = live[u]
-            t["np"] = ps_two.tile([P, PAIR, NKV * DN], F32, name="np")
+            t["np"] = ps_one.tile([P, PAIR, NKV * DN], F32, name="np")
             for i in range(PAIR):
                 nc.tensor.matmul_mx(
                     out=t["np"][:, i, :], lhsT=t["lq"][:, i, :].bitcast(FP8X4), lhsT_scale=t["lqs"][:, i, :],
@@ -237,70 +240,98 @@ def tile_mlacausalselfattention_pa_t_w8_kernel(
                 op=ALU.mult,
             )
 
-        def rope_add(u):
+        def new_kc(u):
+            if "kc" not in live[u]:
+                live[u]["kc"] = keep.tile([P, NH, HD], F32, align_bytes=64, name="lk%d" % (u % 3))
+
+        def rope_add(u, engine=nc.gpsimd):
             t = live[u]
-            t["kr"] = two.tile([P, NH, DR], F32, name="kr")
+            new_kc(u)
             pr = t["pr"][:].rearrange("p i h a (b c) -> p (i h) a b c", b=2)
-            nc.gpsimd.tensor_tensor(
-                t["kr"][:].rearrange("p j (b c) -> p j b c", b=2), pr[:, :, 0], pr[:, :, 1, ::-1, :], op=ALU.add
+            engine.tensor_tensor(
+                t["kc"][:, :, 0:DR].rearrange("p j (b c) -> p j b c", b=2), pr[:, :, 0], pr[:, :, 1, ::-1, :], op=ALU.add
             )
+
+        def copy_nope(u, copy=nc.scalar.copy):
+            t = live[u]
+            new_kc(u)
+            copy(t["kc"][:, :, DR:HD], t["np"][:].rearrange("p i (h d) -> p (i h) d", h=NKV))
 
         def copy_v(u, i, copy=nc.scalar.copy):
             t = live[u]
             if i == 0:
                 t["vo"] = two.tile([P, PAIR, NKV * HD], F32, name="vo")
             copy(t["vo"][:, i, :], t["vp", i][:])
-            if i == PAIR - 1:
-                i0 = (PAIR * u) % RUN
-                nc.sync.dma_start(out=v_v[PAIR * u // RUN][:, i0 : i0 + PAIR, :], in_=t["vo"][:])
 
-        def squares(u, part):
+        def store_v(u, i0=0, i1=PAIR):
+            r0 = (PAIR * u) % RUN
+            nc.sync.dma_start(out=v_v[PAIR * u // RUN][:, r0 + i0 : r0 + i1, :], in_=live[u]["vo"][:, i0:i1, :])
+
+        def squares(u, j0=0, j1=NH - 2 * STAT_PAIRS):
             t = live[u]
             if "ss" not in t:
-                t["ss"] = two.tile([P, NH, 2], F32, name="ss")
-            if part == 0:
-                src = t["kr"][:]
-            else:
-                src = t["np"][:].rearrange("p i (h d) -> p (i h) d", h=NKV)
-            sq = two.tile([P, NH, DR], F32, name="sq")
-            for j in range(NH):
-                nc.scalar.activation(sq[:, j, :], src[:, j, :], ACT.Square, accum_out=t["ss"][:, j, part : part + 1])
+                t["ss"] = two.tile([P, NH], F32, name="ss")
+            sq = two.tile([P, NH, HD], F32, name="sq")
+            for j in range(j0, j1):
+                nc.scalar.activation(sq[:, j, :], t["kc"][:, j, :], ACT.Square, accum_out=t["ss"][:, j : j + 1])
 
-        def sum_halves(u):
+        def squares_vector(u, j0, j1):
             t = live[u]
-            t["st"] = two.tile([P, NH], F32, name="st")
-            nc.vector.tensor_reduce(t["st"][:], t["ss"][:], axis=AXIS.X, op=ALU.add)
+            sq = two.tile([P, NH, HD], F32, name="sqv")
+            for j in range(j0, j1):
+                nc.vector.scalar_tensor_tensor(
+                    out=sq[:, j, :], in0=t["kc"][:, j, :], scalar=1.0, in1=t["kc"][:, j, :], op0=ALU.mult, op1=ALU.mult,
+                    accum_out=t["ss"][:, j : j + 1],
+                )
+
+        def head_stats(u):
+            t = live[u]
+            t["st"] = two.tile([P, STAT_PAIRS, 2, 3], F32, name="st")
+            for b in range(STAT_PAIRS):
+                j = NH - 2 * STAT_PAIRS + 2 * b
+                nc.vector.bn_stats(
+                    t["st"][:, b].rearrange("p e c -> p (e c)"), t["kc"][:, j : j + 2, :].rearrange("p h d -> p d h")
+                )
+
+        def mean_squares(u):
+            st = live[u]["st"][:].rearrange("p b e c -> p (b e) c")
+            nc.scalar.activation(st[:, :, 0], st[:, :, 1], ACT.Square, scale=math.sqrt(HD))
+
+        def sum_stats(u):
+            t = live[u]
+            if "ss" not in t:
+                t["ss"] = two.tile([P, NH], F32, name="ss")
+            st = t["st"][:].rearrange("p b e c -> p (b e) c")
+            nc.vector.tensor_reduce(t["ss"][:, NH - 2 * STAT_PAIRS : NH], st[:, :, 0:3:2], axis=AXIS.X, op=ALU.add)
 
         def inv_root(u):
             t = live[u]
             t["rs"] = two.tile([P, NH], F32, name="rs")
-            nc.scalar.activation(t["rs"][:], t["st"][:], ACT.Abs_reciprocal_sqrt, bias=EPS, scale=1.0 / HD)
+            nc.scalar.activation(t["rs"][:], t["ss"][:], ACT.Abs_reciprocal_sqrt, bias=EPS, scale=1.0 / HD)
 
-        def scale_rope(u):
-            t = live[u]
-            t["ko"] = two.tile([P, NH, HD], F32, name="ko")
-            for j in range(NH):
-                nc.scalar.activation(t["ko"][:, j, 0:DR], t["kr"][:, j, :], ACT.Copy, scale=t["rs"][:, j : j + 1])
+        def new_ko(u):
+            if "ko" not in live[u]:
+                live[u]["ko"] = two.tile([P, NH, HD], F32, name="ko")
 
-        def scale_rope_vector(u):
+        def scale_scalar(u, j0=0, j1=NH - HEADS_V):
             t = live[u]
-            t["ko"] = two.tile([P, NH, HD], F32, name="ko")
-            for j in range(NH):
+            new_ko(u)
+            for j in range(j0, j1):
+                nc.scalar.activation(t["ko"][:, j, :], t["kc"][:, j, :], ACT.Copy, scale=t["rs"][:, j : j + 1])
+
+        def scale_vector(u, j0=NH - HEADS_V, j1=NH):
+            t = live[u]
+            new_ko(u)
+            for j in range(j0, j1):
                 nc.vector.tensor_scalar(
-                    out=t["ko"][:, j, 0:DR], in0=t["kr"][:, j, :], scalar1=t["rs"][:, j : j + 1], scalar2=None, op0=ALU.mult
+                    out=t["ko"][:, j, :], in0=t["kc"][:, j, :], scalar1=t["rs"][:, j : j + 1], scalar2=None, op0=ALU.mult
                 )
 
-        def scale_nope(u):
-            t = live[u]
-            nc.vector.tensor_tensor(
-                t["ko"][:, :, DR:HD],
-                t["np"][:].rearrange("p i (h d) -> p (i h) d", h=NKV),
-                t["rs"][:].unsqueeze(2).to_broadcast([P, NH, DN]),
-                op=ALU.mult,
-            )
-            i0 = (PAIR * u) % RUN
+        def store_k(u, i0=0, i1=PAIR):
+            r0 = (PAIR * u) % RUN
             nc.sync.dma_start(
-                out=k_v[PAIR * u // RUN][:, i0 : i0 + PAIR, :], in_=t["ko"][:].rearrange("p (i h) d -> p i (h d)", i=PAIR)
+                out=k_v[PAIR * u // RUN][:, r0 + i0 : r0 + i1, :],
+                in_=live[u]["ko"][:, NKV * i0 : NKV * i1, :].rearrange("p (i h) d -> p i (h d)", h=NKV),
             )
 
         def run(stage, u, *rest):
@@ -320,72 +351,90 @@ def tile_mlacausalselfattention_pa_t_w8_kernel(
         transposes(0, 1)
 
         for u in range(-1, NU - 1):
-            run(quant_x, u)
+            run(scale_vector, u - 3)
+            run(store_k, u - 3, 1, 2)
             run(quant_lat, u - 1)
+            run(quant_x, u)
+            run(rope_add, u - 1)
             if u >= 0:
                 run(widen, u + 3)
-            run(rope_add, u - 1)
             run(copy_v, u - 2, 0)
+            run(inv_root, u - 2)
             run(copy_v, u - 2, 1)
+            run(store_v, u - 2)
+            run(mm_nope, u - 1)
             run(mm_rope, u)
             run(mm_lat, u, 0)
             run(mm_lat, u, 1)
-            run(squares, u - 2, 0)
-            run(squares, u - 2, 1)
+            run(copy_nope, u - 1)
+            run(scale_scalar, u - 2)
+            run(store_k, u - 2, 0, 1)
             run(copy_x, u + 1, 0)
             run(transposes, u + 2, 0)
-            run(copy_x, u + 1, 1)
-            run(sum_halves, u - 2)
+            run(copy_x, u + 1, 1, (0,))
+            run(head_stats, u - 1)
+            run(squares, u - 1, 0, 3)
             run(copy_lat, u, 0)
-            run(inv_root, u - 2)
+            run(mean_squares, u - 1)
             run(copy_lat, u, 1)
-            run(scale_rope, u - 2)
             if u == 0:
                 build_trig(RUN, NT // 2)
+            run(squares, u - 1, 3)
+            run(copy_x, u + 1, 1, (1,))
+            run(rope_products, u)
+            run(sum_stats, u - 1)
             run(mm_v, u - 1, 0)
             run(mm_v, u - 1, 1)
-            run(mm_nope, u - 1)
-            run(rope_products, u)
             run(transposes, u + 2, 1)
-            run(scale_nope, u - 2)
         quant_x(NU - 1)
         quant_lat(NU - 2)
+        scale_vector(NU - 4)
+        store_k(NU - 4, 1, 2)
         rope_add(NU - 2)
         copy_v(NU - 3, 0)
-        copy_v(NU - 3, 1)
+        store_v(NU - 3, 0, 1)
+        inv_root(NU - 3)
+        copy_v(NU - 3, 1, nc.vector.tensor_copy)
+        store_v(NU - 3, 1, 2)
         mm_lat(NU - 1, 0)
+        mm_nope(NU - 2)
         mm_lat(NU - 1, 1)
         mm_rope(NU - 1)
-        squares(NU - 3, 0)
-        squares(NU - 3, 1)
         mm_v(NU - 2, 0)
         copy_lat(NU - 1, 0, nc.vector.tensor_copy)
-        mm_nope(NU - 2)
-        copy_lat(NU - 1, 1, nc.vector.tensor_copy)
         mm_v(NU - 2, 1)
-        sum_halves(NU - 3)
-        rope_products(NU - 1)
-        inv_root(NU - 3)
-        squares(NU - 2, 0)
+        copy_nope(NU - 2)
+        copy_lat(NU - 1, 1)
+        scale_vector(NU - 3, 0, 4)
+        store_k(NU - 3, 0, 1)
+        scale_vector(NU - 3, 4, 8)
+        store_k(NU - 3, 1, 2)
         quant_lat(NU - 1)
-        rope_add(NU - 1)
-        scale_rope_vector(NU - 3)
-        scale_nope(NU - 3)
-        squares(NU - 2, 1)
+        rope_products(NU - 1)
+        squares(NU - 2, 0, 8)
         mm_nope(NU - 1)
-        copy_v(NU - 2, 0, nc.vector.tensor_copy)
         mm_v(NU - 1, 0)
-        sum_halves(NU - 2)
-        copy_v(NU - 2, 1, nc.vector.tensor_copy)
+        rope_add(NU - 1)
+        copy_v(NU - 2, 0, nc.vector.tensor_copy)
+        store_v(NU - 2, 0, 1)
+        copy_nope(NU - 1)
         inv_root(NU - 2)
+        copy_v(NU - 2, 1, nc.vector.tensor_copy)
+        store_v(NU - 2, 1, 2)
         mm_v(NU - 1, 1)
-        squares(NU - 1, 1)
-        squares(NU - 1, 0)
-        scale_rope_vector(NU - 2)
-        scale_nope(NU - 2)
-        copy_v(NU - 1, 0, nc.vector.tensor_copy)
-        sum_halves(NU - 1)
+        copy_v(NU - 1, 0)
+        store_v(NU - 1, 0, 1)
+        scale_vector(NU - 2, 0, 4)
+        store_k(NU - 2, 0, 1)
+        scale_vector(NU - 2, 4, 8)
+        store_k(NU - 2, 1, 2)
+        squares(NU - 1, 0, 5)
+        squares_vector(NU - 1, 5, 8)
+        copy_v(NU - 1, 1, nc.vector.tensor_copy)
+        store_v(NU - 1, 1, 2)
         inv_root(NU - 1)
-        copy_v(NU - 1, 1)
-        scale_rope_vector(NU - 1)
-        scale_nope(NU - 1)
+        scale_vector(NU - 1, 0, 4)
+        store_k(NU - 1, 0, 1)
+        scale_scalar(NU - 1, 4, 6)
+        scale_vector(NU - 1, 6, 8)
+        store_k(NU - 1, 1, 2)

@@ -57,6 +57,10 @@ def tile_mlacausalselfattention_pa_t_w8_kernel(
         nc.vector.memset(sc_raw[:].bitcast(I32), 0)
         nc.vector.memset(sc_kr[:].bitcast(I32), 0)
         nc.vector.memset(sc_w[:].bitcast(I32), 0)
+        warm_in = keep.tile([P, 1], F32, name="warm_in")
+        warm_out = keep.tile([P, 1], F32, name="warm_out")
+        nc.vector.memset(warm_in[:], 1.0)
+        nc.scalar.activation(warm_out[:], warm_in[:], ACT.Abs_reciprocal_sqrt)
         ident = keep.tile([P, P], F32, name="ident")
         make_identity(nc, ident[:])
 

@@ -75,13 +75,14 @@ def tile_mlacausalselfattention_pa_t_w8_kernel(
         load_x(0, 0, 1)
         xs_scale = keep.tile([P, 2, 4], F32, name="xs_scale")
         nc.sync.dma_start(out=xs_scale[:], in_=x_scale.rearrange("a b (g p t) -> p (a b g) t", p=P, t=4))
-        load_x(0, 1, RUN)
+        load_x(0, 1, 2)
         kv_raw = keep.tile([P, 2, DL], I32, align_bytes=64, name="kv_raw")
         nc.sync.dma_start(out=kv_raw[:], in_=w_kv_words.rearrange("g p n t -> p g (n t)").bitcast(I32))
+        load_x(0, 2, RUN)
         kv_s = w_kv_scales.bitcast(I32)
         for q in range(4):
             nc.sync.dma_start(out=sc_raw[32 * q : 32 * q + 8, :].bitcast(I32), in_=kv_s[:, 4 * q : 4 * q + 4, :])
-        load_x(1, 0, 4)
+        load_x(1, 0, RUN)
         kr_w = keep.tile([P, 2, NKV * DR], I32, align_bytes=64, name="kr_w")
         nc.sync.dma_start(out=kr_w[:], in_=w_krope_words.rearrange("g p n t -> p g (n t)").bitcast(I32))
         kr_s = w_krope_scales.bitcast(I32)
@@ -138,35 +139,40 @@ def tile_mlacausalselfattention_pa_t_w8_kernel(
             new_xs(u)
             nc.gpsimd.tensor_copy(t["xs"][:], x_fp8(PAIR * u, PAIR))
 
-        def transposes(u, i):
-            t = live[u]
-            words = t["xs"][:, C * i : C * (i + 1)].bitcast(F32)
-            t["xt", i] = ps_two.tile([P, 4, P], F32, name="xt")
-            for g in range(2):
-                for w in range(2):
-                    nc.tensor.transpose(t["xt", i][:, 2 * g + w, :], words[:, 256 * g + w : 256 * (g + 1) : 2], ident[:])
+        def turn_words(u, i, g, w, out):
+            words = live[u]["xs"][:, C * i : C * (i + 1)].bitcast(F32)
+            nc.tensor.transpose(out, words[:, 256 * g + w : 256 * (g + 1) : 2], ident[:])
 
-        def copy_x(u, i, passes=(0, 1)):
+        def scale_x(u, g, i0, i1, pairs):
             t = live[u]
             if "xg" not in t:
-                t["xg"] = two.tile([P, PAIR, 2, P, 4], BF16, align_bytes=64, name="xg")
-            pairs = t["xt", i][:].rearrange("p m r -> p (m r)").bitcast(BF16).rearrange("p (g w r e) -> p g r w e", g=2, w=2, e=2)
-            for g in passes:
-                nc.vector.tensor_tensor(
-                    t["xg"][:, i, g].rearrange("p r (w e) -> p r w e", e=2),
-                    pairs[:, g],
-                    xs_scale[:, g].rearrange("p (w e) -> p w e", e=2).unsqueeze(1).to_broadcast([P, P, 2, 2]),
-                    op=ALU.mult,
-                )
+                t["xg"] = two.tile([P, 2, PAIR, P, 4], BF16, align_bytes=64, name="xg")
+            rows = (i1 - i0) * P
+            nc.vector.tensor_tensor(
+                t["xg"][:, g, i0:i1].rearrange("p i r (w e) -> p (i r) w e", e=2),
+                pairs.rearrange("p w r -> p (w r)").bitcast(BF16).rearrange("p (w r e) -> p r w e", w=2, e=2),
+                xs_scale[:, g].rearrange("p (w e) -> p w e", e=2).unsqueeze(1).to_broadcast([P, rows, 2, 2]),
+                op=ALU.mult,
+            )
+
+        def transposes(u, g):
+            t = live[u]
+            t["xt", g] = ps_two.tile([P, 2, PAIR * P], F32, name="xt")
+            for i in range(PAIR):
+                for w in range(2):
+                    turn_words(u, i, g, w, t["xt", g][:, w, P * i : P * (i + 1)])
+
+        def copy_x(u, g):
+            scale_x(u, g, 0, PAIR, live[u]["xt", g][:])
 
         def quant_x(u):
             t = live[u]
-            t["xq"] = two.tile([P, PAIR, 2, P], U32, align_bytes=64, name="xq")
-            t["xqs"] = two.tile([P, PAIR, 2, P], U8, align_bytes=64, name="xqs")
+            t["xq"] = two.tile([P, 2, PAIR, P], U32, align_bytes=64, name="xq")
+            t["xqs"] = two.tile([P, 2, PAIR, P], U8, align_bytes=64, name="xqs")
             nc.vector.quantize_mx(
-                out=t["xq"][:].rearrange("p i g r -> p (i g r)").bitcast(FP8X4),
-                scales=t["xqs"][:].rearrange("p i g r -> p (i g r)"),
-                in_=t["xg"][:].rearrange("p i g r j -> p (i g r j)"),
+                out=t["xq"][:].rearrange("p g i r -> p (g i r)").bitcast(FP8X4),
+                scales=t["xqs"][:].rearrange("p g i r -> p (g i r)"),
+                in_=t["xg"][:].rearrange("p g i r j -> p (g i r j)"),
             )
 
         def mm_lat(u, i):
@@ -178,8 +184,8 @@ def tile_mlacausalselfattention_pa_t_w8_kernel(
                         out=t["lat", i][:, j, :],
                         lhsT=kv_w[:, g, P * j : P * (j + 1)].bitcast(FP8X4),
                         lhsT_scale=sc_kv[4 * g : P, P * j : P * (j + 1)],
-                        rhs=t["xq"][:, i, g, :].bitcast(FP8X4),
-                        rhs_scale=t["xqs"][:, i, g, :],
+                        rhs=t["xq"][:, g, i, :].bitcast(FP8X4),
+                        rhs_scale=t["xqs"][:, g, i, :],
                         start=(g == 0),
                         stop=(g == 1),
                     )
@@ -191,8 +197,8 @@ def tile_mlacausalselfattention_pa_t_w8_kernel(
                 for g in range(2):
                     nc.tensor.matmul_mx(
                         out=t["rp"][:, i, :],
-                        lhsT=t["xq"][:, i, g, :].bitcast(FP8X4),
-                        lhsT_scale=t["xqs"][:, i, g, :],
+                        lhsT=t["xq"][:, g, i, :].bitcast(FP8X4),
+                        lhsT_scale=t["xqs"][:, g, i, :],
                         rhs=kr_w[:, g, :].bitcast(FP8X4),
                         rhs_scale=sc_kr[4 * g : P, :],
                         start=(g == 0),
@@ -342,26 +348,52 @@ def tile_mlacausalselfattention_pa_t_w8_kernel(
             if 0 <= u < NU:
                 stage(u, *rest)
 
-        for u in range(3):
+        def widen_scalar(u, width):
             live[u]["xs"] = keep.tile([P, PAIR * C], BF16, align_bytes=64, name="xs_head%d" % u)
+            for c0 in range(0, C, width):
+                for i in range(PAIR):
+                    nc.scalar.copy(live[u]["xs"][:, C * i + c0 : C * i + c0 + width], x_fp8(PAIR * u + i, 1)[:, c0 : c0 + width])
+
+        live[0]["xs"] = keep.tile([P, PAIR * C], BF16, align_bytes=64, name="xs_head0")
         for n in range(PAIR):
             nc.vector.tensor_copy(live[0]["xs"][:, C * n : C * n + C // 2], x_fp8(n, 1)[:, 0 : C // 2])
             nc.scalar.copy(live[0]["xs"][:, C * n + C // 2 : C * (n + 1)], x_fp8(n, 1)[:, C // 2 : C])
-        for n in range(PAIR, 3 * PAIR):
-            nc.scalar.copy(live[n // PAIR]["xs"][:, C * (n % PAIR) : C * (n % PAIR + 1)], x_fp8(n, 1))
+        widen_scalar(1, C // 2)
         permute_kv()
         build_trig(0, RUN)
-        transposes(0, 0)
-        transposes(0, 1)
+        live[0]["xg"] = keep.tile([P, 2, PAIR, P, 4], BF16, align_bytes=64, name="first")
+        for i in range(PAIR):
+            bank = ps_two.tile([P, 2, 2, P], F32, name="xt")
+            for g in range(2):
+                for w in range(2):
+                    turn_words(0, i, g, w, bank[:, g, w, :])
+            for g in range(2):
+                scale_x(0, g, i, i + 1, bank[:, g])
+        transposes(1, 0)
+        transposes(1, 1)
+        quant_x(0)
+        live[2]["xs"] = keep.tile([P, PAIR * C], BF16, align_bytes=64, name="first")
+        nc.gpsimd.tensor_copy(live[2]["xs"][:], x_fp8(2 * PAIR, PAIR))
+        widen_scalar(3, C)
+        mm_rope(0)
+        mm_lat(0, 0)
+        mm_lat(0, 1)
+        copy_lat(0, 0)
+        copy_lat(0, 1)
+        build_trig(RUN, NT // 2)
+        copy_x(1, 0)
+        copy_x(1, 1)
+        rope_products(0)
+        transposes(2, 0)
+        transposes(2, 1)
 
-        for u in range(-1, NU - 1):
+        for u in range(1, NU - 2):
             run(scale_vector, u - 3)
-            run(store_k, u - 3, 1, 2)
+            run(store_k, u - 3)
             run(quant_lat, u - 1)
             run(quant_x, u)
             run(rope_add, u - 1)
-            if u >= 0:
-                run(widen, u + 3)
+            run(widen, u + 3)
             run(copy_v, u - 2, 0)
             run(inv_root, u - 2)
             run(copy_v, u - 2, 1)
@@ -372,73 +404,91 @@ def tile_mlacausalselfattention_pa_t_w8_kernel(
             run(mm_lat, u, 1)
             run(copy_nope, u - 1)
             run(scale_scalar, u - 2)
-            run(store_k, u - 2, 0, 1)
             run(copy_x, u + 1, 0)
             run(transposes, u + 2, 0)
-            run(copy_x, u + 1, 1, (0,))
+            run(copy_x, u + 1, 1)
             run(head_stats, u - 1)
             run(squares, u - 1, 0, 3)
             run(copy_lat, u, 0)
-            run(mean_squares, u - 1)
             run(copy_lat, u, 1)
-            if u == 0:
-                build_trig(RUN, NT // 2)
+            run(mean_squares, u - 1)
             run(squares, u - 1, 3)
-            run(copy_x, u + 1, 1, (1,))
             run(rope_products, u)
             run(sum_stats, u - 1)
             run(mm_v, u - 1, 0)
             run(mm_v, u - 1, 1)
             run(transposes, u + 2, 1)
+        scale_vector(NU - 5)
+        store_k(NU - 5)
+        quant_lat(NU - 3)
+        quant_x(NU - 2)
+        rope_add(NU - 3)
+        copy_v(NU - 4, 0)
+        inv_root(NU - 4)
+        copy_v(NU - 4, 1)
+        store_v(NU - 4)
+        mm_nope(NU - 3)
+        mm_rope(NU - 2)
+        mm_lat(NU - 2, 0)
+        mm_lat(NU - 2, 1)
+        copy_nope(NU - 3)
+        scale_scalar(NU - 4)
+        copy_x(NU - 1, 0)
+        copy_lat(NU - 2, 0)
+        copy_lat(NU - 2, 1)
+        squares(NU - 3, 0, 8)
+        copy_x(NU - 1, 1)
+        mm_v(NU - 3, 0)
+        mm_v(NU - 3, 1)
+        scale_vector(NU - 4)
+        store_k(NU - 4)
         quant_x(NU - 1)
         quant_lat(NU - 2)
-        scale_vector(NU - 4)
-        store_k(NU - 4, 1, 2)
+        rope_products(NU - 2)
         rope_add(NU - 2)
+        mm_lat(NU - 1, 0)
+        mm_lat(NU - 1, 1)
+        mm_nope(NU - 2)
+        mm_rope(NU - 1)
         copy_v(NU - 3, 0)
         store_v(NU - 3, 0, 1)
         inv_root(NU - 3)
+        mm_v(NU - 2, 0)
+        copy_nope(NU - 2)
+        scale_scalar(NU - 3, 0, 4)
+        store_k(NU - 3, 0, 1)
+        scale_scalar(NU - 3, 4, 8)
+        store_k(NU - 3, 1, 2)
+        copy_lat(NU - 1, 0, nc.vector.tensor_copy)
+        copy_lat(NU - 1, 1, nc.vector.tensor_copy)
+        rope_products(NU - 1)
+        quant_lat(NU - 1)
+        rope_add(NU - 1)
         copy_v(NU - 3, 1, nc.vector.tensor_copy)
         store_v(NU - 3, 1, 2)
-        mm_lat(NU - 1, 0)
-        mm_nope(NU - 2)
-        mm_lat(NU - 1, 1)
-        mm_rope(NU - 1)
-        mm_v(NU - 2, 0)
-        copy_lat(NU - 1, 0, nc.vector.tensor_copy)
         mm_v(NU - 2, 1)
-        copy_nope(NU - 2)
-        copy_lat(NU - 1, 1)
-        scale_vector(NU - 3, 0, 4)
-        store_k(NU - 3, 0, 1)
-        scale_vector(NU - 3, 4, 8)
-        store_k(NU - 3, 1, 2)
-        quant_lat(NU - 1)
-        rope_products(NU - 1)
-        squares(NU - 2, 0, 8)
         mm_nope(NU - 1)
-        mm_v(NU - 1, 0)
-        rope_add(NU - 1)
+        squares(NU - 2, 0, 8)
         copy_v(NU - 2, 0, nc.vector.tensor_copy)
         store_v(NU - 2, 0, 1)
-        copy_nope(NU - 1)
+        mm_v(NU - 1, 0)
         inv_root(NU - 2)
+        copy_nope(NU - 1)
         copy_v(NU - 2, 1, nc.vector.tensor_copy)
         store_v(NU - 2, 1, 2)
         mm_v(NU - 1, 1)
-        copy_v(NU - 1, 0)
-        store_v(NU - 1, 0, 1)
         scale_vector(NU - 2, 0, 4)
         store_k(NU - 2, 0, 1)
         scale_vector(NU - 2, 4, 8)
         store_k(NU - 2, 1, 2)
-        squares(NU - 1, 0, 5)
-        squares_vector(NU - 1, 5, 8)
-        copy_v(NU - 1, 1, nc.vector.tensor_copy)
-        store_v(NU - 1, 1, 2)
+        squares(NU - 1, 0, 6)
+        squares_vector(NU - 1, 6, 8)
+        copy_v(NU - 1, 0, nc.vector.tensor_copy)
+        store_v(NU - 1, 0, 1)
         inv_root(NU - 1)
+        copy_v(NU - 1, 1)
+        store_v(NU - 1, 1, 2)
         scale_vector(NU - 1, 0, 4)
         store_k(NU - 1, 0, 1)
-        scale_scalar(NU - 1, 4, 6)
-        scale_vector(NU - 1, 6, 8)
+        scale_vector(NU - 1, 4, 8)
         store_k(NU - 1, 1, 2)

@@ -54,15 +54,17 @@ def tile_mlacausalselfattention_pa_t_w8_kernel(
         sc_w = keep.tile([P, DL], U8, align_bytes=64, name="sc_w")
         sc_kv = keep.tile([P, DL], U8, align_bytes=64, name="sc_kv")
         sc_kr = keep.tile([P, NKV * DR], U8, align_bytes=64, name="sc_kr")
-        nc.vector.memset(sc_raw[:].bitcast(I32), 0)
-        nc.vector.memset(sc_kr[:].bitcast(I32), 0)
-        nc.vector.memset(sc_w[:].bitcast(I32), 0)
         warm_in = keep.tile([P, 1], F32, name="warm_in")
         warm_out = keep.tile([P, 1], F32, name="warm_out")
         nc.vector.memset(warm_in[:], 1.0)
         nc.scalar.activation(warm_out[:], warm_in[:], ACT.Abs_reciprocal_sqrt)
+        nc.vector.memset(sc_raw[:].bitcast(I32), 0)
+        nc.vector.memset(sc_w[:].bitcast(I32), 0)
+        nc.vector.memset(sc_kr[:].bitcast(I32), 0)
+        ident_b = keep.tile([P, P], BF16, name="ident_b")
+        make_identity(nc, ident_b[:])
         ident = keep.tile([P, P], F32, name="ident")
-        make_identity(nc, ident[:])
+        nc.vector.tensor_copy(ident[:], ident_b[:])
 
         x_rows = {}
 
@@ -72,50 +74,63 @@ def tile_mlacausalselfattention_pa_t_w8_kernel(
             for i in range(i0, i1):
                 x_rows[RUN * s + i] = (xin, i - i0)
 
-        load_x(0, 0, 1)
         xs_scale = keep.tile([P, 2, 4], F32, name="xs_scale")
-        nc.sync.dma_start(out=xs_scale[:], in_=x_scale.rearrange("a b (g p t) -> p (a b g) t", p=P, t=4))
-        load_x(0, 1, 2)
-        kv_raw = keep.tile([P, 2, DL], I32, align_bytes=64, name="kv_raw")
-        nc.sync.dma_start(out=kv_raw[:], in_=w_kv_words.rearrange("g p n t -> p g (n t)").bitcast(I32))
-        load_x(0, 2, RUN)
-        kv_s = w_kv_scales.bitcast(I32)
-        for q in range(4):
-            nc.sync.dma_start(out=sc_raw[32 * q : 32 * q + 8, :].bitcast(I32), in_=kv_s[:, 4 * q : 4 * q + 4, :])
-        load_x(1, 0, RUN)
-        kr_w = keep.tile([P, 2, NKV * DR], I32, align_bytes=64, name="kr_w")
-        nc.sync.dma_start(out=kr_w[:], in_=w_krope_words.rearrange("g p n t -> p g (n t)").bitcast(I32))
-        kr_s = w_krope_scales.bitcast(I32)
-        for q in range(4):
-            nc.sync.dma_start(out=sc_kr[32 * q : 32 * q + 8, :].bitcast(I32), in_=kr_s[:, 4 * q : 4 * q + 4, :])
-        cs_in = keep.tile([P, 2, NT // 2, DR // 2], BF16, name="cs_in")
-        for j, src in enumerate((cos, sin)):
-            nc.sync.dma_start(
-                out=cs_in[:, j].rearrange("p (s i) c -> p s i c", i=RUN),
-                in_=src.rearrange("(s p i) c -> p s i c", p=P, i=RUN),
-            )
+        kv_raw = [keep.tile([P, DL], I32, align_bytes=64, name="kv_raw%d" % g) for g in range(2)]
         vu_w = keep.tile([P, NKV * HD], I32, align_bytes=64, name="vu_w")
-        nc.sync.dma_start(out=vu_w[:], in_=w_vup_words[0].rearrange("p n t -> p (n t)").bitcast(I32))
         ku_w = keep.tile([P, NKV * DN], I32, align_bytes=64, name="ku_w")
-        nc.sync.dma_start(out=ku_w[:], in_=w_kup_words[0].rearrange("p n t -> p (n t)").bitcast(I32))
-        vu_s = w_vup_scales.bitcast(I32)
-        ku_s = w_kup_scales.bitcast(I32)
-        for q in range(4):
-            nc.sync.dma_start(out=sc_w[32 * q : 32 * q + 4, :].bitcast(I32), in_=vu_s[0, 4 * q : 4 * q + 4, :])
-            nc.sync.dma_start(
-                out=sc_w[32 * q + 4 : 32 * q + 8, 0 : NKV * DN].bitcast(I32), in_=ku_s[0, 4 * q : 4 * q + 4, :]
-            )
-        for s in range(2, NLOAD):
+        kr_w = keep.tile([P, 2, NKV * DR], I32, align_bytes=64, name="kr_w")
+        cs_in = keep.tile([P, 2, NT // 2, DR // 2], BF16, name="cs_in")
+
+        def load_scales(plane, row0, scales, engine=nc.sync):
+            rows = 4 * scales.shape[0]
+            for q in range(4):
+                engine.dma_start(
+                    out=plane[32 * q + row0 : 32 * q + row0 + rows, 0 : scales.shape[2]].bitcast(I32),
+                    in_=scales.bitcast(I32)[:, 4 * q : 4 * q + 4, :],
+                )
+
+        def load_words(tile, words):
+            nc.sync.dma_start(out=tile, in_=words.rearrange("p n t -> p (n t)").bitcast(I32))
+
+        def load_trig(s0, s1):
+            for j, src in enumerate((cos, sin)):
+                nc.sync.dma_start(
+                    out=cs_in[:, j, RUN * s0 : RUN * s1].rearrange("p (s i) c -> p s i c", i=RUN),
+                    in_=src.rearrange("(s p i) c -> p s i c", p=P, i=RUN)[:, s0:s1],
+                )
+
+        load_x(0, 0, 1)
+        load_x(0, 1, 2)
+        nc.sync.dma_start(out=xs_scale[:], in_=x_scale.rearrange("a b (g p t) -> p (a b g) t", p=P, t=4))
+        load_x(0, 2, RUN)
+        load_words(kv_raw[0][:], w_kv_words[0])
+        load_words(kv_raw[1][:], w_kv_words[1])
+        load_scales(sc_raw, 0, w_kv_scales)
+        load_x(1, PAIR, RUN)
+        load_x(1, 0, PAIR)
+        load_trig(0, 1)
+        nc.sync.dma_start(out=kr_w[:], in_=w_krope_words.rearrange("g p n t -> p g (n t)").bitcast(I32))
+        load_scales(sc_kr, 0, w_krope_scales)
+        load_words(vu_w[:], w_vup_words[0])
+        load_words(ku_w[:], w_kup_words[0])
+        load_scales(sc_w, 0, w_vup_scales)
+        load_scales(sc_w, 4, w_kup_scales)
+        load_x(2, 0, PAIR)
+        load_x(2, PAIR, RUN)
+        load_trig(1, 4)
+        for s in range(3, NLOAD):
             load_x(s, 0, RUN)
 
         kv_w = keep.tile([P, 2, DL], I32, align_bytes=64, name="kv_w")
         trig = keep.tile([P, NT // 2, 2, 2, DR // 2], BF16, name="trig")
 
-        def permute_kv():
+        def permute_words(g):
             nc.gpsimd.tensor_copy(
-                out=kv_w[:].rearrange("p g (t m) -> p g t m", t=4), in_=kv_raw[:].rearrange("p g (m t) -> p g t m", t=4)
+                out=kv_w[:, g].rearrange("p (t m) -> p t m", t=4), in_=kv_raw[g][:].rearrange("p (m t) -> p t m", t=4)
             )
-            nc.gpsimd.tensor_copy(
+
+        def permute_scales():
+            nc.vector.tensor_copy(
                 out=sc_kv[:].rearrange("p (t m) -> p t m", t=4), in_=sc_raw[:].rearrange("p (m t) -> p t m", t=4)
             )
 
@@ -134,26 +149,21 @@ def tile_mlacausalselfattention_pa_t_w8_kernel(
         def new_xs(u):
             live[u]["xs"] = three.tile([P, PAIR * C], BF16, align_bytes=64, name="xs")
 
-        def widen(u):
+        def widen(u, name=None):
             t = live[u]
-            new_xs(u)
+            if name:
+                t["xs"] = keep.tile([P, PAIR * C], BF16, align_bytes=64, name=name)
+            else:
+                new_xs(u)
             nc.gpsimd.tensor_copy(t["xs"][:], x_fp8(PAIR * u, PAIR))
 
         def turn_words(u, i, g, w, out):
             words = live[u]["xs"][:, C * i : C * (i + 1)].bitcast(F32)
             nc.tensor.transpose(out, words[:, 256 * g + w : 256 * (g + 1) : 2], ident[:])
 
-        def scale_x(u, g, i0, i1, pairs):
-            t = live[u]
-            if "xg" not in t:
-                t["xg"] = two.tile([P, 2, PAIR, P, 4], BF16, align_bytes=64, name="xg")
-            rows = (i1 - i0) * P
-            nc.vector.tensor_tensor(
-                t["xg"][:, g, i0:i1].rearrange("p i r (w e) -> p (i r) w e", e=2),
-                pairs.rearrange("p w r -> p (w r)").bitcast(BF16).rearrange("p (w r e) -> p r w e", w=2, e=2),
-                xs_scale[:, g].rearrange("p (w e) -> p w e", e=2).unsqueeze(1).to_broadcast([P, rows, 2, 2]),
-                op=ALU.mult,
-            )
+        def new_xg(u):
+            if "xg" not in live[u]:
+                live[u]["xg"] = two.tile([P, PAIR, 2, P, 4], BF16, align_bytes=64, name="xg")
 
         def transposes(u, g):
             t = live[u]
@@ -163,16 +173,45 @@ def tile_mlacausalselfattention_pa_t_w8_kernel(
                     turn_words(u, i, g, w, t["xt", g][:, w, P * i : P * (i + 1)])
 
         def copy_x(u, g):
-            scale_x(u, g, 0, PAIR, live[u]["xt", g][:])
-
-        def quant_x(u):
             t = live[u]
-            t["xq"] = two.tile([P, 2, PAIR, P], U32, align_bytes=64, name="xq")
-            t["xqs"] = two.tile([P, 2, PAIR, P], U8, align_bytes=64, name="xqs")
+            new_xg(u)
+            nc.vector.tensor_tensor(
+                t["xg"][:, :, g].rearrange("p i r (w e) -> p i r w e", e=2),
+                t["xt", g][:].rearrange("p w r -> p (w r)").bitcast(BF16).rearrange("p (w i r e) -> p i r w e", w=2, i=PAIR, e=2),
+                xs_scale[:, g].unsqueeze(1).to_broadcast([P, PAIR * P, 4]).rearrange("p (i r) (w e) -> p i r w e", i=PAIR, e=2),
+                op=ALU.mult,
+            )
+
+        def turn_tile(u, i, g0=0, g1=2, pool=ps_two, name="xt"):
+            t = live[u]
+            t["xt", i, g0] = pool.tile([P, g1 - g0, 4, P], BF16, name=name)
+            for g in range(g0, g1):
+                for j in range(4):
+                    k0 = C * i + 512 * g
+                    nc.tensor.matmul(
+                        t["xt", i, g0][:, g - g0, j, :], lhsT=t["xs"][:, k0 + j : k0 + 512 : 4], rhs=ident_b[:],
+                        start=True, stop=True,
+                    )
+
+        def copy_tile(u, i, g0=0, g1=2):
+            t = live[u]
+            new_xg(u)
+            nc.vector.tensor_tensor(
+                t["xg"][:, i, g0:g1],
+                t["xt", i, g0][:].rearrange("p g j r -> p g r j"),
+                xs_scale[:, g0:g1].unsqueeze(2).to_broadcast([P, g1 - g0, P, 4]),
+                op=ALU.mult,
+            )
+
+        def quant_x(u, i0=0, i1=PAIR):
+            t = live[u]
+            if i0 == 0:
+                t["xq"] = two.tile([P, PAIR, 2, P], U32, align_bytes=64, name="xq")
+                t["xqs"] = two.tile([P, PAIR, 2, P], U8, align_bytes=64, name="xqs")
             nc.vector.quantize_mx(
-                out=t["xq"][:].rearrange("p g i r -> p (g i r)").bitcast(FP8X4),
-                scales=t["xqs"][:].rearrange("p g i r -> p (g i r)"),
-                in_=t["xg"][:].rearrange("p g i r j -> p (g i r j)"),
+                out=t["xq"][:, i0:i1].rearrange("p i g r -> p (i g r)").bitcast(FP8X4),
+                scales=t["xqs"][:, i0:i1].rearrange("p i g r -> p (i g r)"),
+                in_=t["xg"][:, i0:i1].rearrange("p i g r j -> p (i g r j)"),
             )
 
         def mm_lat(u, i):
@@ -184,21 +223,22 @@ def tile_mlacausalselfattention_pa_t_w8_kernel(
                         out=t["lat", i][:, j, :],
                         lhsT=kv_w[:, g, P * j : P * (j + 1)].bitcast(FP8X4),
                         lhsT_scale=sc_kv[4 * g : P, P * j : P * (j + 1)],
-                        rhs=t["xq"][:, g, i, :].bitcast(FP8X4),
-                        rhs_scale=t["xqs"][:, g, i, :],
+                        rhs=t["xq"][:, i, g, :].bitcast(FP8X4),
+                        rhs_scale=t["xqs"][:, i, g, :],
                         start=(g == 0),
                         stop=(g == 1),
                     )
 
-        def mm_rope(u):
+        def mm_rope(u, i0=0, i1=PAIR, pool=ps_one, name="rp"):
             t = live[u]
-            t["rp"] = ps_one.tile([P, PAIR, NKV * DR], F32, name="rp")
-            for i in range(PAIR):
+            if i0 == 0:
+                t["rp"] = pool.tile([P, PAIR, NKV * DR], F32, name=name)
+            for i in range(i0, i1):
                 for g in range(2):
                     nc.tensor.matmul_mx(
                         out=t["rp"][:, i, :],
-                        lhsT=t["xq"][:, g, i, :].bitcast(FP8X4),
-                        lhsT_scale=t["xqs"][:, g, i, :],
+                        lhsT=t["xq"][:, i, g, :].bitcast(FP8X4),
+                        lhsT_scale=t["xqs"][:, i, g, :],
                         rhs=kr_w[:, g, :].bitcast(FP8X4),
                         rhs_scale=sc_kr[4 * g : P, :],
                         start=(g == 0),
@@ -211,14 +251,15 @@ def tile_mlacausalselfattention_pa_t_w8_kernel(
                 t["lg"] = keep.tile([P, PAIR, P, 4], BF16, align_bytes=64, name="lk%d" % (u % 3))
             copy(t["lg"][:, i], t["lat", i][:].rearrange("p j r -> p r j"))
 
-        def quant_lat(u):
+        def quant_lat(u, i0=0, i1=PAIR):
             t = live[u]
-            t["lq"] = two.tile([P, PAIR, P], U32, align_bytes=64, name="lq")
-            t["lqs"] = two.tile([P, PAIR, P], U8, align_bytes=64, name="lqs")
+            if i0 == 0:
+                t["lq"] = two.tile([P, PAIR, P], U32, align_bytes=64, name="lq")
+                t["lqs"] = two.tile([P, PAIR, P], U8, align_bytes=64, name="lqs")
             nc.vector.quantize_mx(
-                out=t["lq"][:].rearrange("p i r -> p (i r)").bitcast(FP8X4),
-                scales=t["lqs"][:].rearrange("p i r -> p (i r)"),
-                in_=t["lg"][:].rearrange("p i r j -> p (i r j)"),
+                out=t["lq"][:, i0:i1].rearrange("p i r -> p (i r)").bitcast(FP8X4),
+                scales=t["lqs"][:, i0:i1].rearrange("p i r -> p (i r)"),
+                in_=t["lg"][:, i0:i1].rearrange("p i r j -> p (i r j)"),
             )
 
         def mm_v(u, i):
@@ -229,10 +270,11 @@ def tile_mlacausalselfattention_pa_t_w8_kernel(
                 rhs=vu_w[:].bitcast(FP8X4), rhs_scale=sc_w[:], start=True, stop=True,
             )
 
-        def mm_nope(u):
+        def mm_nope(u, i0=0, i1=PAIR):
             t = live[u]
-            t["np"] = ps_one.tile([P, PAIR, NKV * DN], F32, name="np")
-            for i in range(PAIR):
+            if i0 == 0:
+                t["np"] = ps_one.tile([P, PAIR, NKV * DN], F32, name="np")
+            for i in range(i0, i1):
                 nc.tensor.matmul_mx(
                     out=t["np"][:, i, :], lhsT=t["lq"][:, i, :].bitcast(FP8X4), lhsT_scale=t["lqs"][:, i, :],
                     rhs=ku_w[:].bitcast(FP8X4), rhs_scale=sc_w[4:P, 0 : NKV * DN], start=True, stop=True,
@@ -348,53 +390,78 @@ def tile_mlacausalselfattention_pa_t_w8_kernel(
             if 0 <= u < NU:
                 stage(u, *rest)
 
-        def widen_scalar(u, width):
-            live[u]["xs"] = keep.tile([P, PAIR * C], BF16, align_bytes=64, name="xs_head%d" % u)
-            for c0 in range(0, C, width):
-                for i in range(PAIR):
-                    nc.scalar.copy(live[u]["xs"][:, C * i + c0 : C * i + c0 + width], x_fp8(PAIR * u + i, 1)[:, c0 : c0 + width])
+        def widen_part(copy, u, i, c0=0, c1=C):
+            if "xs" not in live[u]:
+                live[u]["xs"] = keep.tile([P, PAIR * C], BF16, align_bytes=64, name="xs_head%d" % u)
+            copy(live[u]["xs"][:, C * i + c0 : C * i + c1], x_fp8(PAIR * u + i, 1)[:, c0:c1])
 
-        live[0]["xs"] = keep.tile([P, PAIR * C], BF16, align_bytes=64, name="xs_head0")
-        for n in range(PAIR):
-            nc.vector.tensor_copy(live[0]["xs"][:, C * n : C * n + C // 2], x_fp8(n, 1)[:, 0 : C // 2])
-            nc.scalar.copy(live[0]["xs"][:, C * n + C // 2 : C * (n + 1)], x_fp8(n, 1)[:, C // 2 : C])
-        widen_scalar(1, C // 2)
-        permute_kv()
+        widen_part(nc.vector.tensor_copy, 0, 0, 0, C // 2)
+        widen_part(nc.scalar.copy, 0, 0, C // 2, C)
+        widen_part(nc.vector.tensor_copy, 0, 1)
+        permute_words(0)
+        permute_words(1)
+        turn_tile(0, 0, 0, 1, ps_three, "acc")
+        turn_tile(0, 0, 1, 2, ps_three, "acc")
+        turn_tile(0, 1)
+        widen_part(nc.scalar.copy, 1, 0)
+        widen_part(nc.scalar.copy, 1, 1)
+        widen_part(nc.scalar.copy, 3, 0)
         build_trig(0, RUN)
-        live[0]["xg"] = keep.tile([P, 2, PAIR, P, 4], BF16, align_bytes=64, name="first")
-        for i in range(PAIR):
-            bank = ps_two.tile([P, 2, 2, P], F32, name="xt")
-            for g in range(2):
-                for w in range(2):
-                    turn_words(0, i, g, w, bank[:, g, w, :])
-            for g in range(2):
-                scale_x(0, g, i, i + 1, bank[:, g])
-        transposes(1, 0)
-        transposes(1, 1)
+        live[0]["xg"] = keep.tile([P, PAIR, 2, P, 4], BF16, align_bytes=64, name="first")
+        copy_tile(0, 0, 0, 1)
+        copy_tile(0, 0, 1, 2)
+        turn_tile(1, 0)
+        copy_tile(0, 1)
+        permute_scales()
         quant_x(0)
         live[2]["xs"] = keep.tile([P, PAIR * C], BF16, align_bytes=64, name="first")
-        nc.gpsimd.tensor_copy(live[2]["xs"][:], x_fp8(2 * PAIR, PAIR))
-        widen_scalar(3, C)
-        mm_rope(0)
+        widen_part(nc.gpsimd.tensor_copy, 2, 0)
+        widen_part(nc.gpsimd.tensor_copy, 2, 1)
+        turn_tile(1, 1)
         mm_lat(0, 0)
         mm_lat(0, 1)
         copy_lat(0, 0)
         copy_lat(0, 1)
-        build_trig(RUN, NT // 2)
-        copy_x(1, 0)
-        copy_x(1, 1)
+        widen_part(nc.scalar.copy, 3, 1)
+        copy_tile(1, 0)
+        turn_tile(2, 0)
+        mm_rope(0)
+        copy_tile(1, 1)
+        turn_tile(2, 1)
+        quant_lat(0)
+        quant_x(1)
+        new_xs(4)
+        widen_part(nc.gpsimd.tensor_copy, 4, 0)
+        mm_nope(0)
+        mm_v(0, 0)
+        mm_lat(1, 0)
+        mm_lat(1, 1)
         rope_products(0)
-        transposes(2, 0)
-        transposes(2, 1)
+        mm_rope(1)
+        mm_v(0, 1)
+        rope_add(0)
+        widen_part(nc.gpsimd.tensor_copy, 4, 1)
+        copy_nope(0)
+        copy_v(0, 0)
+        copy_lat(1, 0)
+        copy_lat(1, 1)
+        build_trig(RUN, NT // 2)
+        copy_tile(2, 0)
+        transposes(3, 0)
+        copy_tile(2, 1)
+        rope_products(1)
+        squares(0, 0, 8)
+        transposes(3, 1)
 
-        for u in range(1, NU - 2):
+        for u in range(2, NU - 2):
             run(scale_vector, u - 3)
             run(store_k, u - 3)
             run(quant_lat, u - 1)
             run(quant_x, u)
             run(rope_add, u - 1)
             run(widen, u + 3)
-            run(copy_v, u - 2, 0)
+            if u > 2:
+                copy_v(u - 2, 0)
             run(inv_root, u - 2)
             run(copy_v, u - 2, 1)
             run(store_v, u - 2)

@@ -61,10 +61,10 @@ def tile_mlacausalselfattention_pa_t_w8_kernel(
         nc.vector.memset(sc_raw[:].bitcast(I32), 0)
         nc.vector.memset(sc_w[:].bitcast(I32), 0)
         nc.vector.memset(sc_kr[:].bitcast(I32), 0)
-        ident_b = keep.tile([P, P], BF16, name="ident_b")
-        make_identity(nc, ident_b[:])
         ident = keep.tile([P, P], F32, name="ident")
-        nc.vector.tensor_copy(ident[:], ident_b[:])
+        make_identity(nc, ident[:])
+        ident_b = keep.tile([P, P], BF16, name="ident_b")
+        nc.vector.tensor_copy(ident_b[:], ident[:])
 
         x_rows = {}
 
@@ -105,17 +105,17 @@ def tile_mlacausalselfattention_pa_t_w8_kernel(
         load_x(0, 2, RUN)
         load_words(kv_raw[0][:], w_kv_words[0])
         load_words(kv_raw[1][:], w_kv_words[1])
+        load_x(1, 0, PAIR)
         load_scales(sc_raw, 0, w_kv_scales)
         load_x(1, PAIR, RUN)
-        load_x(1, 0, PAIR)
-        load_trig(0, 1)
         nc.sync.dma_start(out=kr_w[:], in_=w_krope_words.rearrange("g p n t -> p g (n t)").bitcast(I32))
         load_scales(sc_kr, 0, w_krope_scales)
-        load_words(vu_w[:], w_vup_words[0])
+        load_trig(0, 1)
         load_words(ku_w[:], w_kup_words[0])
-        load_scales(sc_w, 0, w_vup_scales)
         load_scales(sc_w, 4, w_kup_scales)
         load_x(2, 0, PAIR)
+        load_words(vu_w[:], w_vup_words[0])
+        load_scales(sc_w, 0, w_vup_scales)
         load_x(2, PAIR, RUN)
         load_trig(1, 4)
         for s in range(3, NLOAD):
@@ -139,6 +139,13 @@ def tile_mlacausalselfattention_pa_t_w8_kernel(
             nc.scalar.copy(trig[:, n0:n1, 0, 1, :], cs_in[:, 0, n0:n1])
             nc.scalar.mul(trig[:, n0:n1, 1, 0, :], cs_in[:, 1, n0:n1], -1.0)
             nc.scalar.copy(trig[:, n0:n1, 1, 1, :], cs_in[:, 1, n0:n1])
+
+        def build_trig_vector(n0, n1):
+            nc.vector.tensor_copy(trig[:, n0:n1, 0], cs_in[:, 0, n0:n1].unsqueeze(2).to_broadcast([P, n1 - n0, 2, DR // 2]))
+            nc.vector.tensor_scalar(
+                out=trig[:, n0:n1, 1, 0, :], in0=cs_in[:, 1, n0:n1], scalar1=-1.0, scalar2=None, op0=ALU.mult
+            )
+            nc.vector.tensor_copy(trig[:, n0:n1, 1, 1, :], cs_in[:, 1, n0:n1])
 
         live = [{} for u in range(NU)]
 
@@ -184,22 +191,40 @@ def tile_mlacausalselfattention_pa_t_w8_kernel(
 
         def turn_tile(u, i, g0=0, g1=2, pool=ps_two, name="xt"):
             t = live[u]
-            t["xt", i, g0] = pool.tile([P, g1 - g0, 4, P], BF16, name=name)
+            bank = pool.tile([P, g1 - g0, 2, P], F32, name=name)
             for g in range(g0, g1):
-                for j in range(4):
-                    k0 = C * i + 512 * g
-                    nc.tensor.matmul(
-                        t["xt", i, g0][:, g - g0, j, :], lhsT=t["xs"][:, k0 + j : k0 + 512 : 4], rhs=ident_b[:],
-                        start=True, stop=True,
-                    )
+                t["xt", i, g] = bank[:, g - g0]
+                for w in range(2):
+                    turn_words(u, i, g, w, bank[:, g - g0, w, :])
 
         def copy_tile(u, i, g0=0, g1=2):
             t = live[u]
             new_xg(u)
+            for g in range(g0, g1):
+                nc.vector.tensor_tensor(
+                    t["xg"][:, i, g].rearrange("p r (w e) -> p r w e", e=2),
+                    t["xt", i, g].rearrange("p w r -> p (w r)").bitcast(BF16).rearrange("p (w r e) -> p r w e", w=2, e=2),
+                    xs_scale[:, g].unsqueeze(1).to_broadcast([P, P, 4]).rearrange("p r (w e) -> p r w e", e=2),
+                    op=ALU.mult,
+                )
+
+        def turn_tile_mm(u, i):
+            t = live[u]
+            t["xt", i] = ps_two.tile([P, 2, 4, P], BF16, name="xt")
+            for g in range(2):
+                for j in range(4):
+                    k0 = C * i + 512 * g
+                    nc.tensor.matmul(
+                        t["xt", i][:, g, j, :], lhsT=t["xs"][:, k0 + j : k0 + 512 : 4], rhs=ident_b[:], start=True, stop=True
+                    )
+
+        def copy_tile_mm(u, i):
+            t = live[u]
+            new_xg(u)
             nc.vector.tensor_tensor(
-                t["xg"][:, i, g0:g1],
-                t["xt", i, g0][:].rearrange("p g j r -> p g r j"),
-                xs_scale[:, g0:g1].unsqueeze(2).to_broadcast([P, g1 - g0, P, 4]),
+                t["xg"][:, i],
+                t["xt", i][:].rearrange("p g j r -> p g r j"),
+                xs_scale[:].unsqueeze(2).to_broadcast([P, 2, P, 4]),
                 op=ALU.mult,
             )
 
@@ -247,7 +272,7 @@ def tile_mlacausalselfattention_pa_t_w8_kernel(
 
         def copy_lat(u, i, copy=nc.scalar.copy):
             t = live[u]
-            if i == 0:
+            if "lg" not in t:
                 t["lg"] = keep.tile([P, PAIR, P, 4], BF16, align_bytes=64, name="lk%d" % (u % 3))
             copy(t["lg"][:, i], t["lat", i][:].rearrange("p j r -> p r j"))
 
@@ -280,15 +305,16 @@ def tile_mlacausalselfattention_pa_t_w8_kernel(
                     rhs=ku_w[:].bitcast(FP8X4), rhs_scale=sc_w[4:P, 0 : NKV * DN], start=True, stop=True,
                 )
 
-        def rope_products(u):
+        def rope_products(u, i0=0, i1=PAIR):
             t = live[u]
-            t["pr"] = two.tile([P, PAIR, NKV, 2, DR], F32, name="pr")
-            shape = [P, PAIR, NKV, 2, DR]
+            if i0 == 0:
+                t["pr"] = two.tile([P, PAIR, NKV, 2, DR], F32, name="pr")
+            shape = [P, i1 - i0, NKV, 2, DR]
             n0 = (PAIR * u) % (NT // 2)
             nc.vector.tensor_tensor(
-                t["pr"][:],
-                t["rp"][:].rearrange("p i (h d) -> p i h d", h=NKV).unsqueeze(3).to_broadcast(shape),
-                trig[:, n0 : n0 + PAIR].rearrange("p i a b c -> p i a (b c)").unsqueeze(2).to_broadcast(shape),
+                t["pr"][:, i0:i1],
+                t["rp"][:, i0:i1].rearrange("p i (h d) -> p i h d", h=NKV).unsqueeze(3).to_broadcast(shape),
+                trig[:, n0 + i0 : n0 + i1].rearrange("p i a b c -> p i a (b c)").unsqueeze(2).to_broadcast(shape),
                 op=ALU.mult,
             )
 
@@ -296,23 +322,24 @@ def tile_mlacausalselfattention_pa_t_w8_kernel(
             if "kc" not in live[u]:
                 live[u]["kc"] = keep.tile([P, NH, HD], F32, align_bytes=64, name="lk%d" % (u % 3))
 
-        def rope_add(u, engine=nc.gpsimd):
+        def rope_add(u, i0=0, i1=PAIR, engine=nc.gpsimd):
             t = live[u]
             new_kc(u)
-            pr = t["pr"][:].rearrange("p i h a (b c) -> p (i h) a b c", b=2)
+            pr = t["pr"][:, i0:i1].rearrange("p i h a (b c) -> p (i h) a b c", b=2)
             engine.tensor_tensor(
-                t["kc"][:, :, 0:DR].rearrange("p j (b c) -> p j b c", b=2), pr[:, :, 0], pr[:, :, 1, ::-1, :], op=ALU.add
+                t["kc"][:, NKV * i0 : NKV * i1, 0:DR].rearrange("p j (b c) -> p j b c", b=2),
+                pr[:, :, 0], pr[:, :, 1, ::-1, :], op=ALU.add,
             )
 
-        def copy_nope(u, copy=nc.scalar.copy):
+        def copy_nope(u, i0=0, i1=PAIR, copy=nc.scalar.copy):
             t = live[u]
             new_kc(u)
-            copy(t["kc"][:, :, DR:HD], t["np"][:].rearrange("p i (h d) -> p (i h) d", h=NKV))
+            copy(t["kc"][:, NKV * i0 : NKV * i1, DR:HD], t["np"][:, i0:i1].rearrange("p i (h d) -> p (i h) d", h=NKV))
 
         def copy_v(u, i, copy=nc.scalar.copy):
             t = live[u]
             if i == 0:
-                t["vo"] = two.tile([P, PAIR, NKV * HD], F32, name="vo")
+                t["vo"] = three.tile([P, PAIR, NKV * HD], F32, name="vo")
             copy(t["vo"][:, i, :], t["vp", i][:])
 
         def store_v(u, i0=0, i1=PAIR):
@@ -356,14 +383,15 @@ def tile_mlacausalselfattention_pa_t_w8_kernel(
             st = t["st"][:].rearrange("p b e c -> p (b e) c")
             nc.vector.tensor_reduce(t["ss"][:, NH - 2 * STAT_PAIRS : NH], st[:, :, 0:3:2], axis=AXIS.X, op=ALU.add)
 
-        def inv_root(u):
+        def inv_root(u, j0=0, j1=NH):
             t = live[u]
-            t["rs"] = two.tile([P, NH], F32, name="rs")
-            nc.scalar.activation(t["rs"][:], t["ss"][:], ACT.Abs_reciprocal_sqrt, bias=EPS, scale=1.0 / HD)
+            if j0 == 0:
+                t["rs"] = two.tile([P, NH], F32, name="rs")
+            nc.scalar.activation(t["rs"][:, j0:j1], t["ss"][:, j0:j1], ACT.Abs_reciprocal_sqrt, bias=EPS, scale=1.0 / HD)
 
         def new_ko(u):
             if "ko" not in live[u]:
-                live[u]["ko"] = two.tile([P, NH, HD], F32, name="ko")
+                live[u]["ko"] = three.tile([P, NH, HD], F32, name="ko")
 
         def scale_scalar(u, j0=0, j1=NH - HEADS_V):
             t = live[u]
@@ -403,55 +431,49 @@ def tile_mlacausalselfattention_pa_t_w8_kernel(
         turn_tile(0, 0, 0, 1, ps_three, "acc")
         turn_tile(0, 0, 1, 2, ps_three, "acc")
         turn_tile(0, 1)
-        widen_part(nc.scalar.copy, 1, 0)
-        widen_part(nc.scalar.copy, 1, 1)
-        widen_part(nc.scalar.copy, 3, 0)
-        build_trig(0, RUN)
+        for n in range(PAIR, 3 * PAIR):
+            widen_part(nc.scalar.copy, n // PAIR, n % PAIR)
         live[0]["xg"] = keep.tile([P, PAIR, 2, P, 4], BF16, align_bytes=64, name="first")
-        copy_tile(0, 0, 0, 1)
-        copy_tile(0, 0, 1, 2)
-        turn_tile(1, 0)
+        copy_tile(0, 0)
+        turn_tile_mm(1, 0)
         copy_tile(0, 1)
         permute_scales()
         quant_x(0)
-        live[2]["xs"] = keep.tile([P, PAIR * C], BF16, align_bytes=64, name="first")
-        widen_part(nc.gpsimd.tensor_copy, 2, 0)
-        widen_part(nc.gpsimd.tensor_copy, 2, 1)
-        turn_tile(1, 1)
+        widen(3, "first")
+        turn_tile_mm(1, 1)
         mm_lat(0, 0)
         mm_lat(0, 1)
+        live[0]["lg"] = keep.tile([P, PAIR, P, 4], BF16, align_bytes=64, name="second")
         copy_lat(0, 0)
         copy_lat(0, 1)
-        widen_part(nc.scalar.copy, 3, 1)
-        copy_tile(1, 0)
-        turn_tile(2, 0)
-        mm_rope(0)
-        copy_tile(1, 1)
-        turn_tile(2, 1)
-        quant_lat(0)
+        build_trig(0, RUN)
+        copy_tile_mm(1, 0)
+        copy_tile_mm(1, 1)
+        transposes(2, 0)
+        transposes(2, 1)
         quant_x(1)
-        new_xs(4)
-        widen_part(nc.gpsimd.tensor_copy, 4, 0)
+        quant_lat(0)
+        mm_rope(0)
         mm_nope(0)
-        mm_v(0, 0)
         mm_lat(1, 0)
         mm_lat(1, 1)
+        mm_v(0, 0)
+        widen(4, "second")
+        copy_x(2, 0)
         rope_products(0)
-        mm_rope(1)
         mm_v(0, 1)
+        mm_rope(1)
+        transposes(3, 0)
         rope_add(0)
-        widen_part(nc.gpsimd.tensor_copy, 4, 1)
         copy_nope(0)
-        copy_v(0, 0)
         copy_lat(1, 0)
         copy_lat(1, 1)
-        build_trig(RUN, NT // 2)
-        copy_tile(2, 0)
-        transposes(3, 0)
-        copy_tile(2, 1)
+        copy_v(0, 0)
+        copy_x(2, 1)
         rope_products(1)
         squares(0, 0, 8)
         transposes(3, 1)
+        build_trig_vector(RUN, NT // 2)
 
         for u in range(2, NU - 2):
             run(scale_vector, u - 3)

@@ -54,15 +54,18 @@ def tile_mlacausalselfattention_pa_t_w8_kernel(
         sc_w = keep.tile([P, DL], U8, align_bytes=64, name="sc_w")
         sc_kv = keep.tile([P, DL], U8, align_bytes=64, name="sc_kv")
         sc_kr = keep.tile([P, NKV * DR], U8, align_bytes=64, name="sc_kr")
+        sc_ku = keep.tile([P, NKV * DN], U8, align_bytes=64, name="sc_ku")
         warm_in = keep.tile([P, 1], F32, name="warm_in")
         warm_out = keep.tile([P, 1], F32, name="warm_out")
         nc.vector.memset(warm_in[:], 1.0)
         nc.scalar.activation(warm_out[:], warm_in[:], ACT.Abs_reciprocal_sqrt)
+        ident = keep.tile([P, P], F32, name="ident")
+        nc.vector.memset(ident[:], 0.0)
         nc.vector.memset(sc_raw[:].bitcast(I32), 0)
         nc.vector.memset(sc_w[:].bitcast(I32), 0)
         nc.vector.memset(sc_kr[:].bitcast(I32), 0)
-        ident = keep.tile([P, P], F32, name="ident")
-        make_identity(nc, ident[:])
+        nc.vector.memset(sc_ku[:].bitcast(I32), 0)
+        make_identity(nc, ident[:], nomemset=True)
         ident_b = keep.tile([P, P], BF16, name="ident_b")
         nc.vector.tensor_copy(ident_b[:], ident[:])
 
@@ -81,9 +84,9 @@ def tile_mlacausalselfattention_pa_t_w8_kernel(
         kr_w = keep.tile([P, 2, NKV * DR], I32, align_bytes=64, name="kr_w")
         cs_in = keep.tile([P, 2, NT // 2, DR // 2], BF16, name="cs_in")
 
-        def load_scales(plane, row0, scales, engine=nc.sync):
+        def load_scales(plane, row0, scales, engine=nc.sync, q0=0, q1=4):
             rows = 4 * scales.shape[0]
-            for q in range(4):
+            for q in range(q0, q1):
                 engine.dma_start(
                     out=plane[32 * q + row0 : 32 * q + row0 + rows, 0 : scales.shape[2]].bitcast(I32),
                     in_=scales.bitcast(I32)[:, 4 * q : 4 * q + 4, :],
@@ -105,19 +108,18 @@ def tile_mlacausalselfattention_pa_t_w8_kernel(
         load_x(0, 2, RUN)
         load_words(kv_raw[0][:], w_kv_words[0])
         load_words(kv_raw[1][:], w_kv_words[1])
-        load_x(1, 0, PAIR)
         load_scales(sc_raw, 0, w_kv_scales)
+        load_x(1, 0, PAIR)
         load_x(1, PAIR, RUN)
         nc.sync.dma_start(out=kr_w[:], in_=w_krope_words.rearrange("g p n t -> p g (n t)").bitcast(I32))
         load_scales(sc_kr, 0, w_krope_scales)
-        load_trig(0, 1)
-        load_words(ku_w[:], w_kup_words[0])
-        load_scales(sc_w, 4, w_kup_scales)
+        load_trig(0, 4)
         load_x(2, 0, PAIR)
+        load_words(ku_w[:], w_kup_words[0])
+        load_scales(sc_ku, 0, w_kup_scales)
         load_words(vu_w[:], w_vup_words[0])
         load_scales(sc_w, 0, w_vup_scales)
         load_x(2, PAIR, RUN)
-        load_trig(1, 4)
         for s in range(3, NLOAD):
             load_x(s, 0, RUN)
 
@@ -302,7 +304,7 @@ def tile_mlacausalselfattention_pa_t_w8_kernel(
             for i in range(i0, i1):
                 nc.tensor.matmul_mx(
                     out=t["np"][:, i, :], lhsT=t["lq"][:, i, :].bitcast(FP8X4), lhsT_scale=t["lqs"][:, i, :],
-                    rhs=ku_w[:].bitcast(FP8X4), rhs_scale=sc_w[4:P, 0 : NKV * DN], start=True, stop=True,
+                    rhs=ku_w[:].bitcast(FP8X4), rhs_scale=sc_ku[:], start=True, stop=True,
                 )
 
         def rope_products(u, i0=0, i1=PAIR):
@@ -447,33 +449,34 @@ def tile_mlacausalselfattention_pa_t_w8_kernel(
         copy_lat(0, 0)
         copy_lat(0, 1)
         build_trig(0, RUN)
+        build_trig(RUN, NT // 2)
         copy_tile_mm(1, 0)
         copy_tile_mm(1, 1)
+        mm_rope(0)
         transposes(2, 0)
         transposes(2, 1)
         quant_x(1)
         quant_lat(0)
-        mm_rope(0)
-        mm_nope(0)
+        live[4]["xs"] = keep.tile([P, PAIR * C], BF16, align_bytes=64, name="second")
+        widen_part(nc.gpsimd.tensor_copy, 4, 0)
         mm_lat(1, 0)
+        mm_nope(0)
         mm_lat(1, 1)
-        mm_v(0, 0)
-        widen(4, "second")
-        copy_x(2, 0)
         rope_products(0)
-        mm_v(0, 1)
-        mm_rope(1)
-        transposes(3, 0)
         rope_add(0)
-        copy_nope(0)
+        widen_part(nc.gpsimd.tensor_copy, 4, 1)
+        mm_rope(1)
+        copy_x(2, 0)
+        transposes(3, 0)
         copy_lat(1, 0)
+        copy_nope(0)
         copy_lat(1, 1)
-        copy_v(0, 0)
         copy_x(2, 1)
         rope_products(1)
         squares(0, 0, 8)
+        mm_v(0, 0)
+        mm_v(0, 1)
         transposes(3, 1)
-        build_trig_vector(RUN, NT // 2)
 
         for u in range(2, NU - 2):
             run(scale_vector, u - 3)
@@ -482,8 +485,7 @@ def tile_mlacausalselfattention_pa_t_w8_kernel(
             run(quant_x, u)
             run(rope_add, u - 1)
             run(widen, u + 3)
-            if u > 2:
-                copy_v(u - 2, 0)
+            run(copy_v, u - 2, 0)
             run(inv_root, u - 2)
             run(copy_v, u - 2, 1)
             run(store_v, u - 2)

@@ -59,15 +59,20 @@ def tile_mlacausalselfattention_pa_t_w8_kernel(
         warm_out = keep.tile([P, 1], F32, name="warm_out")
         nc.vector.memset(warm_in[:], 1.0)
         nc.scalar.activation(warm_out[:], warm_in[:], ACT.Abs_reciprocal_sqrt)
-        ident = keep.tile([P, P], F32, name="ident")
-        nc.vector.memset(ident[:], 0.0)
+        warm_b = keep.tile([P, DL], BF16, name="warm_b")
+        nc.vector.memset(warm_b[:], 0.0)
+        warm_bank = ps_one.tile([P, DL], F32, name="rp")
+        for n in range(3):
+            nc.tensor.matmul(warm_bank[:], lhsT=warm_b[:, 0:P], rhs=warm_b[:], start=True, stop=True)
+        ident_b = keep.tile([P, P], BF16, name="ident_b")
+        nc.vector.memset(ident_b[:], 0.0)
         nc.vector.memset(sc_raw[:].bitcast(I32), 0)
+        make_identity(nc, ident_b[:], nomemset=True)
         nc.vector.memset(sc_w[:].bitcast(I32), 0)
         nc.vector.memset(sc_kr[:].bitcast(I32), 0)
         nc.vector.memset(sc_ku[:].bitcast(I32), 0)
-        make_identity(nc, ident[:], nomemset=True)
-        ident_b = keep.tile([P, P], BF16, name="ident_b")
-        nc.vector.tensor_copy(ident_b[:], ident[:])
+        ident = keep.tile([P, P], F32, name="ident")
+        nc.vector.tensor_copy(ident[:], ident_b[:])
 
         x_rows = {}
 
@@ -78,7 +83,7 @@ def tile_mlacausalselfattention_pa_t_w8_kernel(
                 x_rows[RUN * s + i] = (xin, i - i0)
 
         xs_scale = keep.tile([P, 2, 4], F32, name="xs_scale")
-        kv_raw = [keep.tile([P, DL], I32, align_bytes=64, name="kv_raw%d" % g) for g in range(2)]
+        kv_raw = keep.tile([P, 2, DL], I32, align_bytes=64, name="kv_raw")
         vu_w = keep.tile([P, NKV * HD], I32, align_bytes=64, name="vu_w")
         ku_w = keep.tile([P, NKV * DN], I32, align_bytes=64, name="ku_w")
         kr_w = keep.tile([P, 2, NKV * DR], I32, align_bytes=64, name="kr_w")
@@ -106,8 +111,7 @@ def tile_mlacausalselfattention_pa_t_w8_kernel(
         load_x(0, 1, 2)
         nc.sync.dma_start(out=xs_scale[:], in_=x_scale.rearrange("a b (g p t) -> p (a b g) t", p=P, t=4))
         load_x(0, 2, RUN)
-        load_words(kv_raw[0][:], w_kv_words[0])
-        load_words(kv_raw[1][:], w_kv_words[1])
+        nc.sync.dma_start(out=kv_raw[:], in_=w_kv_words.rearrange("g p n t -> p g (n t)").bitcast(I32))
         load_scales(sc_raw, 0, w_kv_scales)
         load_x(1, 0, PAIR)
         load_x(1, PAIR, RUN)
@@ -126,9 +130,9 @@ def tile_mlacausalselfattention_pa_t_w8_kernel(
         kv_w = keep.tile([P, 2, DL], I32, align_bytes=64, name="kv_w")
         trig = keep.tile([P, NT // 2, 2, 2, DR // 2], BF16, name="trig")
 
-        def permute_words(g):
-            nc.gpsimd.tensor_copy(
-                out=kv_w[:, g].rearrange("p (t m) -> p t m", t=4), in_=kv_raw[g][:].rearrange("p (m t) -> p t m", t=4)
+        def permute_words():
+            nc.vector.tensor_copy(
+                out=kv_w[:].rearrange("p g (t m) -> p g m t", t=4), in_=kv_raw[:].rearrange("p g (m t) -> p g m t", t=4)
             )
 
         def permute_scales():
@@ -141,13 +145,6 @@ def tile_mlacausalselfattention_pa_t_w8_kernel(
             nc.scalar.copy(trig[:, n0:n1, 0, 1, :], cs_in[:, 0, n0:n1])
             nc.scalar.mul(trig[:, n0:n1, 1, 0, :], cs_in[:, 1, n0:n1], -1.0)
             nc.scalar.copy(trig[:, n0:n1, 1, 1, :], cs_in[:, 1, n0:n1])
-
-        def build_trig_vector(n0, n1):
-            nc.vector.tensor_copy(trig[:, n0:n1, 0], cs_in[:, 0, n0:n1].unsqueeze(2).to_broadcast([P, n1 - n0, 2, DR // 2]))
-            nc.vector.tensor_scalar(
-                out=trig[:, n0:n1, 1, 0, :], in0=cs_in[:, 1, n0:n1], scalar1=-1.0, scalar2=None, op0=ALU.mult
-            )
-            nc.vector.tensor_copy(trig[:, n0:n1, 1, 1, :], cs_in[:, 1, n0:n1])
 
         live = [{} for u in range(NU)]
 
@@ -193,40 +190,22 @@ def tile_mlacausalselfattention_pa_t_w8_kernel(
 
         def turn_tile(u, i, g0=0, g1=2, pool=ps_two, name="xt"):
             t = live[u]
-            bank = pool.tile([P, g1 - g0, 2, P], F32, name=name)
+            t["xt", i, g0] = pool.tile([P, g1 - g0, 4, P], BF16, name=name)
             for g in range(g0, g1):
-                t["xt", i, g] = bank[:, g - g0]
-                for w in range(2):
-                    turn_words(u, i, g, w, bank[:, g - g0, w, :])
+                for j in range(4):
+                    k0 = C * i + 512 * g
+                    nc.tensor.matmul(
+                        t["xt", i, g0][:, g - g0, j, :], lhsT=t["xs"][:, k0 + j : k0 + 512 : 4], rhs=ident_b[:],
+                        start=True, stop=True,
+                    )
 
         def copy_tile(u, i, g0=0, g1=2):
             t = live[u]
             new_xg(u)
-            for g in range(g0, g1):
-                nc.vector.tensor_tensor(
-                    t["xg"][:, i, g].rearrange("p r (w e) -> p r w e", e=2),
-                    t["xt", i, g].rearrange("p w r -> p (w r)").bitcast(BF16).rearrange("p (w r e) -> p r w e", w=2, e=2),
-                    xs_scale[:, g].unsqueeze(1).to_broadcast([P, P, 4]).rearrange("p r (w e) -> p r w e", e=2),
-                    op=ALU.mult,
-                )
-
-        def turn_tile_mm(u, i):
-            t = live[u]
-            t["xt", i] = ps_two.tile([P, 2, 4, P], BF16, name="xt")
-            for g in range(2):
-                for j in range(4):
-                    k0 = C * i + 512 * g
-                    nc.tensor.matmul(
-                        t["xt", i][:, g, j, :], lhsT=t["xs"][:, k0 + j : k0 + 512 : 4], rhs=ident_b[:], start=True, stop=True
-                    )
-
-        def copy_tile_mm(u, i):
-            t = live[u]
-            new_xg(u)
             nc.vector.tensor_tensor(
-                t["xg"][:, i],
-                t["xt", i][:].rearrange("p g j r -> p g r j"),
-                xs_scale[:].unsqueeze(2).to_broadcast([P, 2, P, 4]),
+                t["xg"][:, i, g0:g1],
+                t["xt", i, g0][:].rearrange("p g j r -> p g r j"),
+                xs_scale[:, g0:g1].unsqueeze(2).to_broadcast([P, g1 - g0, P, 4]),
                 op=ALU.mult,
             )
 
@@ -427,22 +406,20 @@ def tile_mlacausalselfattention_pa_t_w8_kernel(
 
         widen_part(nc.vector.tensor_copy, 0, 0, 0, C // 2)
         widen_part(nc.scalar.copy, 0, 0, C // 2, C)
-        widen_part(nc.vector.tensor_copy, 0, 1)
-        permute_words(0)
-        permute_words(1)
+        for n in range(1, 4 * PAIR):
+            widen_part(nc.scalar.copy, n // PAIR, n % PAIR)
         turn_tile(0, 0, 0, 1, ps_three, "acc")
         turn_tile(0, 0, 1, 2, ps_three, "acc")
         turn_tile(0, 1)
-        for n in range(PAIR, 3 * PAIR):
-            widen_part(nc.scalar.copy, n // PAIR, n % PAIR)
-        live[0]["xg"] = keep.tile([P, PAIR, 2, P, 4], BF16, align_bytes=64, name="first")
-        copy_tile(0, 0)
-        turn_tile_mm(1, 0)
+        turn_tile(1, 0)
+        turn_tile(1, 1, 0, 2, ps_one, "np")
+        copy_tile(0, 0, 0, 1)
+        copy_tile(0, 0, 1, 2)
         copy_tile(0, 1)
+        permute_words()
         permute_scales()
         quant_x(0)
-        widen(3, "first")
-        turn_tile_mm(1, 1)
+        turn_tile(2, 0)
         mm_lat(0, 0)
         mm_lat(0, 1)
         live[0]["lg"] = keep.tile([P, PAIR, P, 4], BF16, align_bytes=64, name="second")
@@ -450,13 +427,12 @@ def tile_mlacausalselfattention_pa_t_w8_kernel(
         copy_lat(0, 1)
         build_trig(0, RUN)
         build_trig(RUN, NT // 2)
-        copy_tile_mm(1, 0)
-        copy_tile_mm(1, 1)
+        copy_tile(1, 0)
+        copy_tile(1, 1)
         mm_rope(0)
-        transposes(2, 0)
-        transposes(2, 1)
-        quant_x(1)
+        turn_tile(2, 1)
         quant_lat(0)
+        quant_x(1)
         live[4]["xs"] = keep.tile([P, PAIR * C], BF16, align_bytes=64, name="second")
         widen_part(nc.gpsimd.tensor_copy, 4, 0)
         mm_lat(1, 0)
@@ -466,12 +442,12 @@ def tile_mlacausalselfattention_pa_t_w8_kernel(
         rope_add(0)
         widen_part(nc.gpsimd.tensor_copy, 4, 1)
         mm_rope(1)
-        copy_x(2, 0)
+        copy_tile(2, 0)
         transposes(3, 0)
         copy_lat(1, 0)
         copy_nope(0)
         copy_lat(1, 1)
-        copy_x(2, 1)
+        copy_tile(2, 1)
         rope_products(1)
         squares(0, 0, 8)
         mm_v(0, 0)

@@ -1,4 +1,3 @@
-import math
 from contextlib import ExitStack
 
 import concourse.mybir as mybir
@@ -28,8 +27,8 @@ NLOAD = NT // RUN
 PAIR = 2
 NU = NT // PAIR
 NH = PAIR * NKV
-STAT_PAIRS = 1
-HEADS_V = 3
+WIDE_S = 288
+HEADS_V = 6
 
 
 def tile_mlacausalselfattention_pa_t_w8_kernel(
@@ -161,7 +160,12 @@ def tile_mlacausalselfattention_pa_t_w8_kernel(
                 t["xs"] = keep.tile([P, PAIR * C], BF16, align_bytes=64, name=name)
             else:
                 new_xs(u)
-            nc.gpsimd.tensor_copy(t["xs"][:], x_fp8(PAIR * u, PAIR))
+            cut = PAIR * C - WIDE_S
+            nc.gpsimd.tensor_copy(t["xs"][:, 0:cut], x_fp8(PAIR * u, PAIR)[:, 0:cut])
+
+        def widen_rest(u):
+            cut = PAIR * C - WIDE_S
+            nc.scalar.copy(live[u]["xs"][:, cut:], x_fp8(PAIR * u, PAIR)[:, cut:])
 
         def turn_words(u, i, g, w, out):
             words = live[u]["xs"][:, C * i : C * (i + 1)].bitcast(F32)
@@ -327,7 +331,7 @@ def tile_mlacausalselfattention_pa_t_w8_kernel(
             r0 = (PAIR * u) % RUN
             nc.sync.dma_start(out=v_v[PAIR * u // RUN][:, r0 + i0 : r0 + i1, :], in_=live[u]["vo"][:, i0:i1, :])
 
-        def squares(u, j0=0, j1=NH - 2 * STAT_PAIRS):
+        def squares(u, j0=0, j1=NH):
             t = live[u]
             if "ss" not in t:
                 t["ss"] = two.tile([P, NH], F32, name="ss")
@@ -343,26 +347,6 @@ def tile_mlacausalselfattention_pa_t_w8_kernel(
                     out=sq[:, j, :], in0=t["kc"][:, j, :], scalar=1.0, in1=t["kc"][:, j, :], op0=ALU.mult, op1=ALU.mult,
                     accum_out=t["ss"][:, j : j + 1],
                 )
-
-        def head_stats(u):
-            t = live[u]
-            t["st"] = two.tile([P, STAT_PAIRS, 2, 3], F32, name="st")
-            for b in range(STAT_PAIRS):
-                j = NH - 2 * STAT_PAIRS + 2 * b
-                nc.vector.bn_stats(
-                    t["st"][:, b].rearrange("p e c -> p (e c)"), t["kc"][:, j : j + 2, :].rearrange("p h d -> p d h")
-                )
-
-        def mean_squares(u):
-            st = live[u]["st"][:].rearrange("p b e c -> p (b e) c")
-            nc.scalar.activation(st[:, :, 0], st[:, :, 1], ACT.Square, scale=math.sqrt(HD))
-
-        def sum_stats(u):
-            t = live[u]
-            if "ss" not in t:
-                t["ss"] = two.tile([P, NH], F32, name="ss")
-            st = t["st"][:].rearrange("p b e c -> p (b e) c")
-            nc.vector.tensor_reduce(t["ss"][:, NH - 2 * STAT_PAIRS : NH], st[:, :, 0:3:2], axis=AXIS.X, op=ALU.add)
 
         def inv_root(u, j0=0, j1=NH):
             t = live[u]
@@ -471,91 +455,93 @@ def tile_mlacausalselfattention_pa_t_w8_kernel(
             run(mm_lat, u, 1)
             run(copy_nope, u - 1)
             run(scale_scalar, u - 2)
+            run(widen_rest, u + 3)
             run(copy_x, u + 1, 0)
             run(transposes, u + 2, 0)
             run(copy_x, u + 1, 1)
-            run(head_stats, u - 1)
-            run(squares, u - 1, 0, 3)
+            run(squares, u - 1, 0, 4)
             run(copy_lat, u, 0)
             run(copy_lat, u, 1)
-            run(mean_squares, u - 1)
-            run(squares, u - 1, 3)
+            run(squares, u - 1, 4)
             run(rope_products, u)
-            run(sum_stats, u - 1)
             run(mm_v, u - 1, 0)
             run(mm_v, u - 1, 1)
             run(transposes, u + 2, 1)
-        scale_vector(NU - 5)
-        store_k(NU - 5)
-        quant_lat(NU - 3)
-        quant_x(NU - 2)
-        rope_add(NU - 3)
-        copy_v(NU - 4, 0)
-        inv_root(NU - 4)
-        copy_v(NU - 4, 1)
-        store_v(NU - 4)
-        mm_nope(NU - 3)
-        mm_rope(NU - 2)
-        mm_lat(NU - 2, 0)
-        mm_lat(NU - 2, 1)
-        copy_nope(NU - 3)
-        scale_scalar(NU - 4)
-        copy_x(NU - 1, 0)
-        copy_lat(NU - 2, 0)
-        copy_lat(NU - 2, 1)
-        squares(NU - 3, 0, 8)
-        copy_x(NU - 1, 1)
-        mm_v(NU - 3, 0)
-        mm_v(NU - 3, 1)
-        scale_vector(NU - 4)
-        store_k(NU - 4)
-        quant_x(NU - 1)
-        quant_lat(NU - 2)
-        rope_products(NU - 2)
-        rope_add(NU - 2)
-        mm_lat(NU - 1, 0)
-        mm_lat(NU - 1, 1)
-        mm_nope(NU - 2)
-        mm_rope(NU - 1)
-        copy_v(NU - 3, 0)
-        store_v(NU - 3, 0, 1)
-        inv_root(NU - 3)
-        mm_v(NU - 2, 0)
-        copy_nope(NU - 2)
-        scale_scalar(NU - 3, 0, 4)
-        store_k(NU - 3, 0, 1)
-        scale_scalar(NU - 3, 4, 8)
-        store_k(NU - 3, 1, 2)
-        copy_lat(NU - 1, 0, nc.vector.tensor_copy)
-        copy_lat(NU - 1, 1, nc.vector.tensor_copy)
-        rope_products(NU - 1)
-        quant_lat(NU - 1)
-        rope_add(NU - 1)
-        copy_v(NU - 3, 1, nc.vector.tensor_copy)
-        store_v(NU - 3, 1, 2)
-        mm_v(NU - 2, 1)
-        mm_nope(NU - 1)
-        squares(NU - 2, 0, 8)
-        copy_v(NU - 2, 0, nc.vector.tensor_copy)
-        store_v(NU - 2, 0, 1)
-        mm_v(NU - 1, 0)
-        inv_root(NU - 2)
-        copy_nope(NU - 1)
-        copy_v(NU - 2, 1, nc.vector.tensor_copy)
-        store_v(NU - 2, 1, 2)
-        mm_v(NU - 1, 1)
-        scale_vector(NU - 2, 0, 4)
-        store_k(NU - 2, 0, 1)
-        scale_vector(NU - 2, 4, 8)
-        store_k(NU - 2, 1, 2)
-        squares(NU - 1, 0, 6)
-        squares_vector(NU - 1, 6, 8)
-        copy_v(NU - 1, 0, nc.vector.tensor_copy)
-        store_v(NU - 1, 0, 1)
-        inv_root(NU - 1)
-        copy_v(NU - 1, 1)
-        store_v(NU - 1, 1, 2)
-        scale_vector(NU - 1, 0, 4)
-        store_k(NU - 1, 0, 1)
-        scale_vector(NU - 1, 4, 8)
-        store_k(NU - 1, 1, 2)
+        a, b, c = NU - 3, NU - 2, NU - 1
+        vcopy = nc.vector.tensor_copy
+        scale_vector(a - 2)
+        store_k(a - 2)
+        quant_lat(a)
+        quant_x(b)
+        rope_add(a)
+        copy_v(a - 1, 0)
+        inv_root(a - 1)
+        copy_v(a - 1, 1)
+        store_v(a - 1)
+        mm_nope(a)
+        mm_rope(b)
+        mm_lat(b, 0)
+        mm_lat(b, 1)
+        copy_nope(a)
+        scale_scalar(a - 1)
+        copy_x(c, 0)
+        copy_lat(b, 0)
+        copy_lat(b, 1)
+        copy_x(c, 1)
+        mm_v(a, 0)
+        mm_v(a, 1)
+        scale_vector(a - 1)
+        store_k(a - 1)
+        copy_v(a, 0)
+        store_v(a, 0, 1)
+        squares(a, 0, 8)
+        quant_x(c)
+        quant_lat(b)
+        rope_products(b)
+        rope_add(b)
+        mm_lat(c, 0)
+        mm_lat(c, 1)
+        mm_rope(c, 0, PAIR, ps_two, "xt")
+        mm_nope(b)
+        inv_root(a)
+        copy_v(a, 1, vcopy)
+        store_v(a, 1, 2)
+        mm_v(b, 0)
+        mm_v(b, 1)
+        copy_lat(c, 0)
+        copy_lat(c, 1)
+        rope_products(c)
+        scale_vector(a, 0, 4)
+        store_k(a, 0, 1)
+        scale_vector(a, 4, 8)
+        store_k(a, 1, 2)
+        quant_lat(c)
+        rope_add(c)
+        copy_nope(b)
+        squares(b, 0, 8)
+        mm_nope(c)
+        copy_v(b, 0, vcopy)
+        store_v(b, 0, 1)
+        mm_v(c, 0)
+        copy_v(b, 1, vcopy)
+        store_v(b, 1, 2)
+        mm_v(c, 1)
+        inv_root(b)
+        copy_nope(c)
+        copy_v(c, 0, vcopy)
+        store_v(c, 0, 1)
+        copy_v(c, 1)
+        store_v(c, 1, 2)
+        scale_vector(b, 0, 4)
+        store_k(b, 0, 1)
+        scale_vector(b, 4, 8)
+        store_k(b, 1, 2)
+        squares(c, 0, 4)
+        inv_root(c, 0, 4)
+        squares_vector(c, 5, 8)
+        squares(c, 4, 5)
+        scale_vector(c, 0, 4)
+        store_k(c, 0, 1)
+        inv_root(c, 4, 8)
+        scale_vector(c, 4, 8)
+        store_k(c, 1, 2)

@@ -24,11 +24,17 @@ P = 128
 RUN = 4
 NT = TOK // P
 NLOAD = NT // RUN
+PER_BATCH = NLOAD // B
 PAIR = 2
 NU = NT // PAIR
 NH = PAIR * NKV
-WIDE_S = 288
-HEADS_V = 6
+EARLY = 10
+LATE = (NT - EARLY) * C
+CUT3 = 1536
+LEAD_S = 2048
+LEAD = LEAD_S + 1664
+WIDE_G = 1712
+HEADS_S = (2, 3)
 
 
 def tile_mlacausalselfattention_pa_t_w8_kernel(
@@ -36,9 +42,10 @@ def tile_mlacausalselfattention_pa_t_w8_kernel(
     w_vup_words, w_vup_scales, w_krope_words, w_krope_scales, out_k, out_v,
 ):
     nc = tc.nc
-    x_v = x_bytes.rearrange("b t k -> (b t) k").rearrange("(s p i) k -> s p i k", p=P, i=RUN)
-    k_v = out_k.rearrange("b t h d -> (b t) (h d)").rearrange("(s p i) c -> s p i c", p=P, i=RUN)
-    v_v = out_v.rearrange("b t h d -> (b t) (h d)").rearrange("(s p i) c -> s p i c", p=P, i=RUN)
+    x_v = x_bytes.rearrange("b (p s i) k -> b s p i k", p=P, i=RUN)
+    k_v = out_k.rearrange("b (p s i) h d -> b s p i (h d)", p=P, i=RUN)
+    v_v = out_v.rearrange("b (p s i) h d -> b s p i (h d)", p=P, i=RUN)
+    x_v, k_v, v_v = ([ap[s // PER_BATCH, s % PER_BATCH] for s in range(NLOAD)] for ap in (x_v, k_v, v_v))
 
     with ExitStack() as ctx:
         keep = ctx.enter_context(tc.tile_pool(name="keep", bufs=1))
@@ -75,11 +82,20 @@ def tile_mlacausalselfattention_pa_t_w8_kernel(
 
         x_rows = {}
 
+        x_late = keep.tile([P, LATE], U8, align_bytes=64, name="x_late")
+        xs_late = keep.tile([P, LATE], BF16, align_bytes=64, name="xs_late")
+
         def load_x(s, i0, i1):
-            xin = keep.tile([P, i1 - i0, C], U8, align_bytes=64, name="xin%d_%d" % (s, i0))
-            nc.sync.dma_start(out=xin[:], in_=x_v[s][:, i0:i1, :])
-            for i in range(i0, i1):
-                x_rows[RUN * s + i] = (xin, i - i0)
+            if RUN * s + i0 < EARLY:
+                xin = keep.tile([P, i1 - i0, C], U8, align_bytes=64, name="xin%d_%d" % (s, i0))
+                nc.sync.dma_start(out=xin[:], in_=x_v[s][:, i0:i1, :])
+                for i in range(i0, i1):
+                    x_rows[RUN * s + i] = (xin, i - i0)
+            else:
+                c0 = C * (RUN * s - EARLY)
+                nc.sync.dma_start(
+                    out=x_late[:, c0 + C * i0 : c0 + C * i1], in_=x_v[s][:, i0:i1, :].rearrange("p i k -> p (i k)")
+                )
 
         xs_scale = keep.tile([P, 2, 4], F32, name="xs_scale")
         kv_raw = keep.tile([P, 2, DL], I32, align_bytes=64, name="kv_raw")
@@ -102,28 +118,29 @@ def tile_mlacausalselfattention_pa_t_w8_kernel(
         def load_trig(s0, s1):
             for j, src in enumerate((cos, sin)):
                 nc.sync.dma_start(
-                    out=cs_in[:, j, RUN * s0 : RUN * s1].rearrange("p (s i) c -> p s i c", i=RUN),
-                    in_=src.rearrange("(s p i) c -> p s i c", p=P, i=RUN)[:, s0:s1],
+                    out=cs_in[:, j, RUN * s0 : RUN * s1], in_=src.rearrange("(p n) c -> p n c", p=P)[:, RUN * s0 : RUN * s1]
                 )
 
         load_x(0, 0, 1)
         load_x(0, 1, 2)
         nc.sync.dma_start(out=xs_scale[:], in_=x_scale.rearrange("a b (g p t) -> p (a b g) t", p=P, t=4))
         load_x(0, 2, RUN)
+        load_x(1, 0, PAIR)
         nc.sync.dma_start(out=kv_raw[:], in_=w_kv_words.rearrange("g p n t -> p g (n t)").bitcast(I32))
         load_scales(sc_raw, 0, w_kv_scales)
-        load_x(1, 0, PAIR)
+        load_trig(0, 4)
         load_x(1, PAIR, RUN)
         nc.sync.dma_start(out=kr_w[:], in_=w_krope_words.rearrange("g p n t -> p g (n t)").bitcast(I32))
         load_scales(sc_kr, 0, w_krope_scales)
-        load_trig(0, 4)
         load_x(2, 0, PAIR)
+        load_x(2, PAIR, RUN)
         load_words(ku_w[:], w_kup_words[0])
         load_scales(sc_ku, 0, w_kup_scales)
+        load_x(3, 0, PAIR)
         load_words(vu_w[:], w_vup_words[0])
         load_scales(sc_w, 0, w_vup_scales)
-        load_x(2, PAIR, RUN)
-        for s in range(3, NLOAD):
+        load_x(3, PAIR, RUN)
+        for s in range(4, NLOAD):
             load_x(s, 0, RUN)
 
         kv_w = keep.tile([P, 2, DL], I32, align_bytes=64, name="kv_w")
@@ -151,21 +168,18 @@ def tile_mlacausalselfattention_pa_t_w8_kernel(
             xin, row = x_rows[n]
             return xin[:, row : row + count, :].rearrange("p i k -> p (i k)").bitcast(FP8)
 
-        def new_xs(u):
-            live[u]["xs"] = three.tile([P, PAIR * C], BF16, align_bytes=64, name="xs")
+        for u in range(EARLY // PAIR, NU):
+            c0 = (PAIR * u - EARLY) * C
+            live[u]["xs"] = xs_late[:, c0 : c0 + PAIR * C]
 
-        def widen(u, name=None):
-            t = live[u]
-            if name:
-                t["xs"] = keep.tile([P, PAIR * C], BF16, align_bytes=64, name=name)
-            else:
-                new_xs(u)
-            cut = PAIR * C - WIDE_S
-            nc.gpsimd.tensor_copy(t["xs"][:, 0:cut], x_fp8(PAIR * u, PAIR)[:, 0:cut])
+        def widen_late(copy, c0, c1):
+            c1 = min(c1, LATE)
+            if c0 < c1:
+                copy(xs_late[:, c0:c1], x_late[:, c0:c1].bitcast(FP8))
 
-        def widen_rest(u):
-            cut = PAIR * C - WIDE_S
-            nc.scalar.copy(live[u]["xs"][:, cut:], x_fp8(PAIR * u, PAIR)[:, cut:])
+        def widen(u):
+            c0 = LEAD + (u - 2) * WIDE_G
+            widen_late(nc.gpsimd.tensor_copy, c0, c0 + WIDE_G)
 
         def turn_words(u, i, g, w, out):
             words = live[u]["xs"][:, C * i : C * (i + 1)].bitcast(F32)
@@ -354,18 +368,23 @@ def tile_mlacausalselfattention_pa_t_w8_kernel(
                 t["rs"] = two.tile([P, NH], F32, name="rs")
             nc.scalar.activation(t["rs"][:, j0:j1], t["ss"][:, j0:j1], ACT.Abs_reciprocal_sqrt, bias=EPS, scale=1.0 / HD)
 
+        def heads_scalar(u):
+            return HEADS_S[u % len(HEADS_S)]
+
         def new_ko(u):
             if "ko" not in live[u]:
                 live[u]["ko"] = three.tile([P, NH, HD], F32, name="ko")
 
-        def scale_scalar(u, j0=0, j1=NH - HEADS_V):
+        def scale_scalar(u, j0=0, j1=None):
             t = live[u]
+            j1 = heads_scalar(u) if j1 is None else j1
             new_ko(u)
             for j in range(j0, j1):
                 nc.scalar.activation(t["ko"][:, j, :], t["kc"][:, j, :], ACT.Copy, scale=t["rs"][:, j : j + 1])
 
-        def scale_vector(u, j0=NH - HEADS_V, j1=NH):
+        def scale_vector(u, j0=None, j1=NH):
             t = live[u]
+            j0 = heads_scalar(u) if j0 is None else j0
             new_ko(u)
             for j in range(j0, j1):
                 nc.vector.tensor_scalar(
@@ -388,55 +407,59 @@ def tile_mlacausalselfattention_pa_t_w8_kernel(
                 live[u]["xs"] = keep.tile([P, PAIR * C], BF16, align_bytes=64, name="xs_head%d" % u)
             copy(live[u]["xs"][:, C * i + c0 : C * i + c1], x_fp8(PAIR * u + i, 1)[:, c0:c1])
 
-        widen_part(nc.vector.tensor_copy, 0, 0, 0, C // 2)
-        widen_part(nc.scalar.copy, 0, 0, C // 2, C)
-        for n in range(1, 4 * PAIR):
+        for c0 in range(0, C, C // 2):
+            widen_part(nc.vector.tensor_copy, 0, 0, c0, c0 + C // 4)
+            widen_part(nc.scalar.copy, 0, 0, c0 + C // 4, c0 + C // 2)
+        for n in range(1, 3 * PAIR):
             widen_part(nc.scalar.copy, n // PAIR, n % PAIR)
+        build_trig(0, NT // 2)
         turn_tile(0, 0, 0, 1, ps_three, "acc")
         turn_tile(0, 0, 1, 2, ps_three, "acc")
         turn_tile(0, 1)
         turn_tile(1, 0)
         turn_tile(1, 1, 0, 2, ps_one, "np")
+        live[0]["xg"] = keep.tile([P, PAIR, 2, P, 4], BF16, align_bytes=64, name="first")
         copy_tile(0, 0, 0, 1)
         copy_tile(0, 0, 1, 2)
         copy_tile(0, 1)
+        turn_tile(2, 0)
         permute_words()
         permute_scales()
         quant_x(0)
-        turn_tile(2, 0)
+        live[3]["xs"] = keep.tile([P, PAIR * C], BF16, align_bytes=64, name="first")
+        nc.gpsimd.tensor_copy(live[3]["xs"][:, 0:CUT3], x_fp8(3 * PAIR, PAIR)[:, 0:CUT3])
         mm_lat(0, 0)
         mm_lat(0, 1)
-        live[0]["lg"] = keep.tile([P, PAIR, P, 4], BF16, align_bytes=64, name="second")
         copy_lat(0, 0)
         copy_lat(0, 1)
-        build_trig(0, RUN)
-        build_trig(RUN, NT // 2)
+        nc.scalar.copy(live[3]["xs"][:, CUT3:], x_fp8(3 * PAIR, PAIR)[:, CUT3:])
+        widen_part(nc.scalar.copy, 4, 0)
+        widen_part(nc.scalar.copy, 4, 1)
+        widen_late(nc.scalar.copy, 0, LEAD_S)
         copy_tile(1, 0)
         copy_tile(1, 1)
         mm_rope(0)
         turn_tile(2, 1)
         quant_lat(0)
         quant_x(1)
-        live[4]["xs"] = keep.tile([P, PAIR * C], BF16, align_bytes=64, name="second")
-        widen_part(nc.gpsimd.tensor_copy, 4, 0)
         mm_lat(1, 0)
-        mm_nope(0)
         mm_lat(1, 1)
+        mm_nope(0)
         rope_products(0)
         rope_add(0)
-        widen_part(nc.gpsimd.tensor_copy, 4, 1)
+        widen_late(nc.gpsimd.tensor_copy, LEAD_S, LEAD)
         mm_rope(1)
         copy_tile(2, 0)
         transposes(3, 0)
         copy_lat(1, 0)
-        copy_nope(0)
         copy_lat(1, 1)
+        copy_nope(0)
         copy_tile(2, 1)
         rope_products(1)
         squares(0, 0, 8)
+        transposes(3, 1)
         mm_v(0, 0)
         mm_v(0, 1)
-        transposes(3, 1)
 
         for u in range(2, NU - 2):
             run(scale_vector, u - 3)
@@ -444,7 +467,7 @@ def tile_mlacausalselfattention_pa_t_w8_kernel(
             run(quant_lat, u - 1)
             run(quant_x, u)
             run(rope_add, u - 1)
-            run(widen, u + 3)
+            widen(u)
             run(copy_v, u - 2, 0)
             run(inv_root, u - 2)
             run(copy_v, u - 2, 1)
@@ -455,7 +478,6 @@ def tile_mlacausalselfattention_pa_t_w8_kernel(
             run(mm_lat, u, 1)
             run(copy_nope, u - 1)
             run(scale_scalar, u - 2)
-            run(widen_rest, u + 3)
             run(copy_x, u + 1, 0)
             run(transposes, u + 2, 0)
             run(copy_x, u + 1, 1)

@@ -501,67 +501,70 @@ def tile_mlacausalselfattention_pa_t_w8_kernel(
         copy_v(a - 1, 1)
         store_v(a - 1)
         mm_nope(a)
-        mm_rope(b)
         mm_lat(b, 0)
         mm_lat(b, 1)
-        copy_nope(a)
-        scale_scalar(a - 1)
-        copy_x(c, 0)
-        copy_lat(b, 0)
-        copy_lat(b, 1)
-        copy_x(c, 1)
         mm_v(a, 0)
+        mm_rope(b)
         mm_v(a, 1)
-        scale_vector(a - 1)
-        store_k(a - 1)
+        copy_nope(a)
+        copy_lat(b, 0)
+        squares(a, 0, 4)
+        copy_lat(b, 1)
+        inv_root(a, 0, 4)
         copy_v(a, 0)
         store_v(a, 0, 1)
-        squares(a, 0, 8)
+        squares(a, 4, 8)
+        copy_x(c, 0)
+        copy_x(c, 1)
+        scale_vector(a - 1, 0, 8)
+        store_k(a - 1)
         quant_x(c)
         quant_lat(b)
-        rope_products(b)
-        rope_add(b)
-        mm_lat(c, 0)
-        mm_lat(c, 1)
-        mm_rope(c, 0, PAIR, ps_two, "xt")
-        mm_nope(b)
-        inv_root(a)
-        copy_v(a, 1, vcopy)
-        store_v(a, 1, 2)
-        mm_v(b, 0)
-        mm_v(b, 1)
-        copy_lat(c, 0)
-        copy_lat(c, 1)
-        rope_products(c)
         scale_vector(a, 0, 4)
         store_k(a, 0, 1)
-        scale_vector(a, 4, 8)
-        store_k(a, 1, 2)
-        quant_lat(c)
-        rope_add(c)
-        copy_nope(b)
-        squares(b, 0, 8)
-        mm_nope(c)
-        copy_v(b, 0, vcopy)
+        rope_products(b)
+        rope_add(b)
+        copy_v(a, 1)
+        store_v(a, 1, 2)
+        mm_lat(c, 0)
+        mm_v(b, 0)
+        mm_rope(c, 0, PAIR, ps_two, "xt")
+        mm_nope(b)
+        mm_lat(c, 1)
+        mm_v(b, 1)
+        copy_lat(c, 0)
+        inv_root(a, 4, 8)
+        copy_v(b, 0)
         store_v(b, 0, 1)
-        mm_v(c, 0)
+        copy_nope(b)
+        copy_lat(c, 1)
+        rope_products(c)
         copy_v(b, 1, vcopy)
         store_v(b, 1, 2)
+        quant_lat(c)
+        scale_vector(a, 4, 8)
+        store_k(a, 1, 2)
+        rope_add(c, 0, PAIR, nc.vector)
+        mm_nope(c)
+        mm_v(c, 0)
         mm_v(c, 1)
-        inv_root(b)
-        copy_nope(c)
-        copy_v(c, 0, vcopy)
-        store_v(c, 0, 1)
-        copy_v(c, 1)
-        store_v(c, 1, 2)
+        squares(b, 0, 6)
+        inv_root(b, 0, 4)
+        squares(b, 6, 8)
         scale_vector(b, 0, 4)
         store_k(b, 0, 1)
+        copy_nope(c)
+        inv_root(b, 4, 8)
+        copy_v(c, 0, vcopy)
+        store_v(c, 0, 1)
         scale_vector(b, 4, 8)
         store_k(b, 1, 2)
-        squares(c, 0, 4)
+        squares(c, 0, 6)
+        copy_v(c, 1, vcopy)
+        store_v(c, 1, 2)
         inv_root(c, 0, 4)
-        squares_vector(c, 5, 8)
-        squares(c, 4, 5)
+        squares_vector(c, 7, 8)
+        squares(c, 6, 7)
         scale_vector(c, 0, 4)
         store_k(c, 0, 1)
         inv_root(c, 4, 8)

from contextlib import ExitStack

import concourse.mybir as mybir
from concourse.masks import make_identity

B, T, C, DL = 2, 2048, 1024, 512
NKV, HD, DR, DN = 4, 128, 64, 64
TOK = B * T
EPS = 1.1920928955078125e-07
FLOPS = 2 * TOK * (C * DL + DL * NKV * DN + DL * NKV * HD + C * NKV * DR)

F32 = mybir.dt.float32
BF16 = mybir.dt.bfloat16
I32 = mybir.dt.int32
U32 = mybir.dt.uint32
U8 = mybir.dt.uint8
FP8 = mybir.dt.float8_e4m3fn
FP8X4 = mybir.dt.float8_e4m3fn_x4
ACT = mybir.ActivationFunctionType
ALU = mybir.AluOpType
AXIS = mybir.AxisListType

P = 128
RUN = 4
NT = TOK // P
NLOAD = NT // RUN
PER_BATCH = NLOAD // B
PAIR = 2
NU = NT // PAIR
NH = PAIR * NKV
EARLY = 10
LATE = (NT - EARLY) * C
CUT3 = 1536
LEAD_S = 2048
LEAD = LEAD_S + 1664
WIDE_G = 1712
HEADS_S = (2, 3)


def tile_mlacausalselfattention_pa_t_w8_kernel(
    tc, x_bytes, x_scale, cos, sin, w_kv_words, w_kv_scales, w_kup_words, w_kup_scales,
    w_vup_words, w_vup_scales, w_krope_words, w_krope_scales, out_k, out_v,
):
    nc = tc.nc
    x_v = x_bytes.rearrange("b (p s i) k -> b s p i k", p=P, i=RUN)
    k_v = out_k.rearrange("b (p s i) h d -> b s p i (h d)", p=P, i=RUN)
    v_v = out_v.rearrange("b (p s i) h d -> b s p i (h d)", p=P, i=RUN)
    x_v, k_v, v_v = ([ap[s // PER_BATCH, s % PER_BATCH] for s in range(NLOAD)] for ap in (x_v, k_v, v_v))

    with ExitStack() as ctx:
        keep = ctx.enter_context(tc.tile_pool(name="keep", bufs=1))
        two = ctx.enter_context(tc.tile_pool(name="two", bufs=2))
        three = ctx.enter_context(tc.tile_pool(name="three", bufs=3))
        ps_one = ctx.enter_context(tc.psum_pool(name="ps_one", bufs=1))
        ps_two = ctx.enter_context(tc.psum_pool(name="ps_two", bufs=2))
        ps_three = ctx.enter_context(tc.psum_pool(name="ps_three", bufs=4))
        ctx.enter_context(tc.manual_schedule())

        sc_raw = keep.tile([P, DL], U8, align_bytes=64, name="sc_raw")
        sc_w = keep.tile([P, DL], U8, align_bytes=64, name="sc_w")
        sc_kv = keep.tile([P, DL], U8, align_bytes=64, name="sc_kv")
        sc_kr = keep.tile([P, NKV * DR], U8, align_bytes=64, name="sc_kr")
        sc_ku = keep.tile([P, NKV * DN], U8, align_bytes=64, name="sc_ku")
        warm_in = keep.tile([P, 1], F32, name="warm_in")
        warm_out = keep.tile([P, 1], F32, name="warm_out")
        nc.vector.memset(warm_in[:], 1.0)
        nc.scalar.activation(warm_out[:], warm_in[:], ACT.Abs_reciprocal_sqrt)
        warm_b = keep.tile([P, DL], BF16, name="warm_b")
        nc.vector.memset(warm_b[:], 0.0)
        warm_bank = ps_one.tile([P, DL], F32, name="rp")
        for n in range(3):
            nc.tensor.matmul(warm_bank[:], lhsT=warm_b[:, 0:P], rhs=warm_b[:], start=True, stop=True)
        ident_b = keep.tile([P, P], BF16, name="ident_b")
        nc.vector.memset(ident_b[:], 0.0)
        nc.vector.memset(sc_raw[:].bitcast(I32), 0)
        make_identity(nc, ident_b[:], nomemset=True)
        nc.vector.memset(sc_w[:].bitcast(I32), 0)
        nc.vector.memset(sc_kr[:].bitcast(I32), 0)
        nc.vector.memset(sc_ku[:].bitcast(I32), 0)
        ident = keep.tile([P, P], F32, name="ident")
        nc.vector.tensor_copy(ident[:], ident_b[:])

        x_rows = {}

        x_late = keep.tile([P, LATE], U8, align_bytes=64, name="x_late")
        xs_late = keep.tile([P, LATE], BF16, align_bytes=64, name="xs_late")

        def load_x(s, i0, i1):
            if RUN * s + i0 < EARLY:
                xin = keep.tile([P, i1 - i0, C], U8, align_bytes=64, name="xin%d_%d" % (s, i0))
                nc.sync.dma_start(out=xin[:], in_=x_v[s][:, i0:i1, :])
                for i in range(i0, i1):
                    x_rows[RUN * s + i] = (xin, i - i0)
            else:
                c0 = C * (RUN * s - EARLY)
                nc.sync.dma_start(
                    out=x_late[:, c0 + C * i0 : c0 + C * i1], in_=x_v[s][:, i0:i1, :].rearrange("p i k -> p (i k)")
                )

        xs_scale = keep.tile([P, 2, 4], F32, name="xs_scale")
        kv_raw = keep.tile([P, 2, DL], I32, align_bytes=64, name="kv_raw")
        vu_w = keep.tile([P, NKV * HD], I32, align_bytes=64, name="vu_w")
        ku_w = keep.tile([P, NKV * DN], I32, align_bytes=64, name="ku_w")
        kr_w = keep.tile([P, 2, NKV * DR], I32, align_bytes=64, name="kr_w")
        cs_in = keep.tile([P, 2, NT // 2, DR // 2], BF16, name="cs_in")

        def load_scales(plane, row0, scales, engine=nc.sync, q0=0, q1=4):
            rows = 4 * scales.shape[0]
            for q in range(q0, q1):
                engine.dma_start(
                    out=plane[32 * q + row0 : 32 * q + row0 + rows, 0 : scales.shape[2]].bitcast(I32),
                    in_=scales.bitcast(I32)[:, 4 * q : 4 * q + 4, :],
                )

        def load_words(tile, words):
            nc.sync.dma_start(out=tile, in_=words.rearrange("p n t -> p (n t)").bitcast(I32))

        def load_trig(s0, s1):
            for j, src in enumerate((cos, sin)):
                nc.sync.dma_start(
                    out=cs_in[:, j, RUN * s0 : RUN * s1], in_=src.rearrange("(p n) c -> p n c", p=P)[:, RUN * s0 : RUN * s1]
                )

        load_x(0, 0, 1)
        load_x(0, 1, 2)
        nc.sync.dma_start(out=xs_scale[:], in_=x_scale.rearrange("a b (g p t) -> p (a b g) t", p=P, t=4))
        load_x(0, 2, RUN)
        load_x(1, 0, PAIR)
        nc.sync.dma_start(out=kv_raw[:], in_=w_kv_words.rearrange("g p n t -> p g (n t)").bitcast(I32))
        load_scales(sc_raw, 0, w_kv_scales)
        load_trig(0, 4)
        load_x(1, PAIR, RUN)
        nc.sync.dma_start(out=kr_w[:], in_=w_krope_words.rearrange("g p n t -> p g (n t)").bitcast(I32))
        load_scales(sc_kr, 0, w_krope_scales)
        load_x(2, 0, PAIR)
        load_x(2, PAIR, RUN)
        load_words(ku_w[:], w_kup_words[0])
        load_scales(sc_ku, 0, w_kup_scales)
        load_x(3, 0, PAIR)
        load_words(vu_w[:], w_vup_words[0])
        load_scales(sc_w, 0, w_vup_scales)
        load_x(3, PAIR, RUN)
        for s in range(4, NLOAD):
            load_x(s, 0, RUN)

        kv_w = keep.tile([P, 2, DL], I32, align_bytes=64, name="kv_w")
        trig = keep.tile([P, NT // 2, 2, 2, DR // 2], BF16, name="trig")

        def permute_words():
            nc.vector.tensor_copy(
                out=kv_w[:].rearrange("p g (t m) -> p g m t", t=4), in_=kv_raw[:].rearrange("p g (m t) -> p g m t", t=4)
            )

        def permute_scales():
            nc.vector.tensor_copy(
                out=sc_kv[:].rearrange("p (t m) -> p t m", t=4), in_=sc_raw[:].rearrange("p (m t) -> p t m", t=4)
            )

        def build_trig(n0, n1):
            nc.scalar.copy(trig[:, n0:n1, 0, 0, :], cs_in[:, 0, n0:n1])
            nc.scalar.copy(trig[:, n0:n1, 0, 1, :], cs_in[:, 0, n0:n1])
            nc.scalar.mul(trig[:, n0:n1, 1, 0, :], cs_in[:, 1, n0:n1], -1.0)
            nc.scalar.copy(trig[:, n0:n1, 1, 1, :], cs_in[:, 1, n0:n1])

        live = [{} for u in range(NU)]

        def x_fp8(n, count):
            xin, row = x_rows[n]
            return xin[:, row : row + count, :].rearrange("p i k -> p (i k)").bitcast(FP8)

        for u in range(EARLY // PAIR, NU):
            c0 = (PAIR * u - EARLY) * C
            live[u]["xs"] = xs_late[:, c0 : c0 + PAIR * C]

        def widen_late(copy, c0, c1):
            c1 = min(c1, LATE)
            if c0 < c1:
                copy(xs_late[:, c0:c1], x_late[:, c0:c1].bitcast(FP8))

        def widen(u):
            c0 = LEAD + (u - 2) * WIDE_G
            widen_late(nc.gpsimd.tensor_copy, c0, c0 + WIDE_G)

        def turn_words(u, i, g, w, out):
            words = live[u]["xs"][:, C * i : C * (i + 1)].bitcast(F32)
            nc.tensor.transpose(out, words[:, 256 * g + w : 256 * (g + 1) : 2], ident[:])

        def new_xg(u):
            if "xg" not in live[u]:
                live[u]["xg"] = two.tile([P, PAIR, 2, P, 4], BF16, align_bytes=64, name="xg")

        def transposes(u, g):
            t = live[u]
            t["xt", g] = ps_two.tile([P, 2, PAIR * P], F32, name="xt")
            for i in range(PAIR):
                for w in range(2):
                    turn_words(u, i, g, w, t["xt", g][:, w, P * i : P * (i + 1)])

        def copy_x(u, g):
            t = live[u]
            new_xg(u)
            nc.vector.tensor_tensor(
                t["xg"][:, :, g].rearrange("p i r (w e) -> p i r w e", e=2),
                t["xt", g][:].rearrange("p w r -> p (w r)").bitcast(BF16).rearrange("p (w i r e) -> p i r w e", w=2, i=PAIR, e=2),
                xs_scale[:, g].unsqueeze(1).to_broadcast([P, PAIR * P, 4]).rearrange("p (i r) (w e) -> p i r w e", i=PAIR, e=2),
                op=ALU.mult,
            )

        def turn_tile(u, i, g0=0, g1=2, pool=ps_two, name="xt"):
            t = live[u]
            t["xt", i, g0] = pool.tile([P, g1 - g0, 4, P], BF16, name=name)
            for g in range(g0, g1):
                for j in range(4):
                    k0 = C * i + 512 * g
                    nc.tensor.matmul(
                        t["xt", i, g0][:, g - g0, j, :], lhsT=t["xs"][:, k0 + j : k0 + 512 : 4], rhs=ident_b[:],
                        start=True, stop=True,
                    )

        def copy_tile(u, i, g0=0, g1=2):
            t = live[u]
            new_xg(u)
            nc.vector.tensor_tensor(
                t["xg"][:, i, g0:g1],
                t["xt", i, g0][:].rearrange("p g j r -> p g r j"),
                xs_scale[:, g0:g1].unsqueeze(2).to_broadcast([P, g1 - g0, P, 4]),
                op=ALU.mult,
            )

        def quant_x(u, i0=0, i1=PAIR):
            t = live[u]
            if i0 == 0:
                t["xq"] = two.tile([P, PAIR, 2, P], U32, align_bytes=64, name="xq")
                t["xqs"] = two.tile([P, PAIR, 2, P], U8, align_bytes=64, name="xqs")
            nc.vector.quantize_mx(
                out=t["xq"][:, i0:i1].rearrange("p i g r -> p (i g r)").bitcast(FP8X4),
                scales=t["xqs"][:, i0:i1].rearrange("p i g r -> p (i g r)"),
                in_=t["xg"][:, i0:i1].rearrange("p i g r j -> p (i g r j)"),
            )

        def mm_lat(u, i):
            t = live[u]
            t["lat", i] = ps_three.tile([P, 4, P], F32, name="acc")
            for j in range(4):
                for g in range(2):
                    nc.tensor.matmul_mx(
                        out=t["lat", i][:, j, :],
                        lhsT=kv_w[:, g, P * j : P * (j + 1)].bitcast(FP8X4),
                        lhsT_scale=sc_kv[4 * g : P, P * j : P * (j + 1)],
                        rhs=t["xq"][:, i, g, :].bitcast(FP8X4),
                        rhs_scale=t["xqs"][:, i, g, :],
                        start=(g == 0),
                        stop=(g == 1),
                    )

        def mm_rope(u, i0=0, i1=PAIR, pool=ps_one, name="rp"):
            t = live[u]
            if i0 == 0:
                t["rp"] = pool.tile([P, PAIR, NKV * DR], F32, name=name)
            for i in range(i0, i1):
                for g in range(2):
                    nc.tensor.matmul_mx(
                        out=t["rp"][:, i, :],
                        lhsT=t["xq"][:, i, g, :].bitcast(FP8X4),
                        lhsT_scale=t["xqs"][:, i, g, :],
                        rhs=kr_w[:, g, :].bitcast(FP8X4),
                        rhs_scale=sc_kr[4 * g : P, :],
                        start=(g == 0),
                        stop=(g == 1),
                    )

        def copy_lat(u, i, copy=nc.scalar.copy):
            t = live[u]
            if "lg" not in t:
                t["lg"] = keep.tile([P, PAIR, P, 4], BF16, align_bytes=64, name="lk%d" % (u % 3))
            copy(t["lg"][:, i], t["lat", i][:].rearrange("p j r -> p r j"))

        def quant_lat(u, i0=0, i1=PAIR):
            t = live[u]
            if i0 == 0:
                t["lq"] = two.tile([P, PAIR, P], U32, align_bytes=64, name="lq")
                t["lqs"] = two.tile([P, PAIR, P], U8, align_bytes=64, name="lqs")
            nc.vector.quantize_mx(
                out=t["lq"][:, i0:i1].rearrange("p i r -> p (i r)").bitcast(FP8X4),
                scales=t["lqs"][:, i0:i1].rearrange("p i r -> p (i r)"),
                in_=t["lg"][:, i0:i1].rearrange("p i r j -> p (i r j)"),
            )

        def mm_v(u, i):
            t = live[u]
            t["vp", i] = ps_three.tile([P, NKV * HD], F32, name="acc")
            nc.tensor.matmul_mx(
                out=t["vp", i][:], lhsT=t["lq"][:, i, :].bitcast(FP8X4), lhsT_scale=t["lqs"][:, i, :],
                rhs=vu_w[:].bitcast(FP8X4), rhs_scale=sc_w[:], start=True, stop=True,
            )

        def mm_nope(u, i0=0, i1=PAIR):
            t = live[u]
            if i0 == 0:
                t["np"] = ps_one.tile([P, PAIR, NKV * DN], F32, name="np")
            for i in range(i0, i1):
                nc.tensor.matmul_mx(
                    out=t["np"][:, i, :], lhsT=t["lq"][:, i, :].bitcast(FP8X4), lhsT_scale=t["lqs"][:, i, :],
                    rhs=ku_w[:].bitcast(FP8X4), rhs_scale=sc_ku[:], start=True, stop=True,
                )

        def rope_products(u, i0=0, i1=PAIR):
            t = live[u]
            if i0 == 0:
                t["pr"] = two.tile([P, PAIR, NKV, 2, DR], F32, name="pr")
            shape = [P, i1 - i0, NKV, 2, DR]
            n0 = (PAIR * u) % (NT // 2)
            nc.vector.tensor_tensor(
                t["pr"][:, i0:i1],
                t["rp"][:, i0:i1].rearrange("p i (h d) -> p i h d", h=NKV).unsqueeze(3).to_broadcast(shape),
                trig[:, n0 + i0 : n0 + i1].rearrange("p i a b c -> p i a (b c)").unsqueeze(2).to_broadcast(shape),
                op=ALU.mult,
            )

        def new_kc(u):
            if "kc" not in live[u]:
                live[u]["kc"] = keep.tile([P, NH, HD], F32, align_bytes=64, name="lk%d" % (u % 3))

        def rope_add(u, i0=0, i1=PAIR, engine=nc.gpsimd):
            t = live[u]
            new_kc(u)
            pr = t["pr"][:, i0:i1].rearrange("p i h a (b c) -> p (i h) a b c", b=2)
            engine.tensor_tensor(
                t["kc"][:, NKV * i0 : NKV * i1, 0:DR].rearrange("p j (b c) -> p j b c", b=2),
                pr[:, :, 0], pr[:, :, 1, ::-1, :], op=ALU.add,
            )

        def copy_nope(u, i0=0, i1=PAIR, copy=nc.scalar.copy):
            t = live[u]
            new_kc(u)
            copy(t["kc"][:, NKV * i0 : NKV * i1, DR:HD], t["np"][:, i0:i1].rearrange("p i (h d) -> p (i h) d", h=NKV))

        def copy_v(u, i, copy=nc.scalar.copy):
            t = live[u]
            if i == 0:
                t["vo"] = three.tile([P, PAIR, NKV * HD], F32, name="vo")
            copy(t["vo"][:, i, :], t["vp", i][:])

        def store_v(u, i0=0, i1=PAIR):
            r0 = (PAIR * u) % RUN
            nc.sync.dma_start(out=v_v[PAIR * u // RUN][:, r0 + i0 : r0 + i1, :], in_=live[u]["vo"][:, i0:i1, :])

        def squares(u, j0=0, j1=NH):
            t = live[u]
            if "ss" not in t:
                t["ss"] = two.tile([P, NH], F32, name="ss")
            sq = two.tile([P, NH, HD], F32, name="sq")
            for j in range(j0, j1):
                nc.scalar.activation(sq[:, j, :], t["kc"][:, j, :], ACT.Square, accum_out=t["ss"][:, j : j + 1])

        def squares_vector(u, j0, j1):
            t = live[u]
            sq = two.tile([P, NH, HD], F32, name="sqv")
            for j in range(j0, j1):
                nc.vector.scalar_tensor_tensor(
                    out=sq[:, j, :], in0=t["kc"][:, j, :], scalar=1.0, in1=t["kc"][:, j, :], op0=ALU.mult, op1=ALU.mult,
                    accum_out=t["ss"][:, j : j + 1],
                )

        def inv_root(u, j0=0, j1=NH):
            t = live[u]
            if j0 == 0:
                t["rs"] = two.tile([P, NH], F32, name="rs")
            nc.scalar.activation(t["rs"][:, j0:j1], t["ss"][:, j0:j1], ACT.Abs_reciprocal_sqrt, bias=EPS, scale=1.0 / HD)

        def heads_scalar(u):
            return HEADS_S[u % len(HEADS_S)]

        def new_ko(u):
            if "ko" not in live[u]:
                live[u]["ko"] = three.tile([P, NH, HD], F32, name="ko")

        def scale_scalar(u, j0=0, j1=None):
            t = live[u]
            j1 = heads_scalar(u) if j1 is None else j1
            new_ko(u)
            for j in range(j0, j1):
                nc.scalar.activation(t["ko"][:, j, :], t["kc"][:, j, :], ACT.Copy, scale=t["rs"][:, j : j + 1])

        def scale_vector(u, j0=None, j1=NH):
            t = live[u]
            j0 = heads_scalar(u) if j0 is None else j0
            new_ko(u)
            for j in range(j0, j1):
                nc.vector.tensor_scalar(
                    out=t["ko"][:, j, :], in0=t["kc"][:, j, :], scalar1=t["rs"][:, j : j + 1], scalar2=None, op0=ALU.mult
                )

        def store_k(u, i0=0, i1=PAIR):
            r0 = (PAIR * u) % RUN
            nc.sync.dma_start(
                out=k_v[PAIR * u // RUN][:, r0 + i0 : r0 + i1, :],
                in_=live[u]["ko"][:, NKV * i0 : NKV * i1, :].rearrange("p (i h) d -> p i (h d)", h=NKV),
            )

        def run(stage, u, *rest):
            if 0 <= u < NU:
                stage(u, *rest)

        def widen_part(copy, u, i, c0=0, c1=C):
            if "xs" not in live[u]:
                live[u]["xs"] = keep.tile([P, PAIR * C], BF16, align_bytes=64, name="xs_head%d" % u)
            copy(live[u]["xs"][:, C * i + c0 : C * i + c1], x_fp8(PAIR * u + i, 1)[:, c0:c1])

        for c0 in range(0, C, C // 2):
            widen_part(nc.vector.tensor_copy, 0, 0, c0, c0 + C // 4)
            widen_part(nc.scalar.copy, 0, 0, c0 + C // 4, c0 + C // 2)
        for n in range(1, 3 * PAIR):
            widen_part(nc.scalar.copy, n // PAIR, n % PAIR)
        build_trig(0, NT // 2)
        turn_tile(0, 0, 0, 1, ps_three, "acc")
        turn_tile(0, 0, 1, 2, ps_three, "acc")
        turn_tile(0, 1)
        turn_tile(1, 0)
        turn_tile(1, 1, 0, 2, ps_one, "np")
        live[0]["xg"] = keep.tile([P, PAIR, 2, P, 4], BF16, align_bytes=64, name="first")
        copy_tile(0, 0, 0, 1)
        copy_tile(0, 0, 1, 2)
        copy_tile(0, 1)
        turn_tile(2, 0)
        permute_words()
        permute_scales()
        quant_x(0)
        live[3]["xs"] = keep.tile([P, PAIR * C], BF16, align_bytes=64, name="first")
        nc.gpsimd.tensor_copy(live[3]["xs"][:, 0:CUT3], x_fp8(3 * PAIR, PAIR)[:, 0:CUT3])
        mm_lat(0, 0)
        mm_lat(0, 1)
        copy_lat(0, 0)
        copy_lat(0, 1)
        nc.scalar.copy(live[3]["xs"][:, CUT3:], x_fp8(3 * PAIR, PAIR)[:, CUT3:])
        widen_part(nc.scalar.copy, 4, 0)
        widen_part(nc.scalar.copy, 4, 1)
        widen_late(nc.scalar.copy, 0, LEAD_S)
        copy_tile(1, 0)
        copy_tile(1, 1)
        mm_rope(0)
        turn_tile(2, 1)
        quant_lat(0)
        quant_x(1)
        mm_lat(1, 0)
        mm_lat(1, 1)
        mm_nope(0)
        rope_products(0)
        rope_add(0)
        widen_late(nc.gpsimd.tensor_copy, LEAD_S, LEAD)
        mm_rope(1)
        copy_tile(2, 0)
        transposes(3, 0)
        copy_lat(1, 0)
        copy_lat(1, 1)
        copy_nope(0)
        copy_tile(2, 1)
        rope_products(1)
        squares(0, 0, 8)
        transposes(3, 1)
        mm_v(0, 0)
        mm_v(0, 1)

        for u in range(2, NU - 2):
            run(scale_vector, u - 3)
            run(store_k, u - 3)
            run(quant_lat, u - 1)
            run(quant_x, u)
            run(rope_add, u - 1)
            widen(u)
            run(copy_v, u - 2, 0)
            run(inv_root, u - 2)
            run(copy_v, u - 2, 1)
            run(store_v, u - 2)
            run(mm_nope, u - 1)
            run(mm_rope, u)
            run(mm_lat, u, 0)
            run(mm_lat, u, 1)
            run(copy_nope, u - 1)
            run(scale_scalar, u - 2)
            run(copy_x, u + 1, 0)
            run(transposes, u + 2, 0)
            run(copy_x, u + 1, 1)
            run(squares, u - 1, 0, 4)
            run(copy_lat, u, 0)
            run(copy_lat, u, 1)
            run(squares, u - 1, 4)
            run(rope_products, u)
            run(mm_v, u - 1, 0)
            run(mm_v, u - 1, 1)
            run(transposes, u + 2, 1)
        a, b, c = NU - 3, NU - 2, NU - 1
        vcopy = nc.vector.tensor_copy
        scale_vector(a - 2)
        store_k(a - 2)
        quant_lat(a)
        quant_x(b)
        rope_add(a)
        copy_v(a - 1, 0)
        inv_root(a - 1)
        copy_v(a - 1, 1)
        store_v(a - 1)
        mm_nope(a)
        mm_lat(b, 0)
        mm_lat(b, 1)
        mm_v(a, 0)
        mm_rope(b)
        mm_v(a, 1)
        copy_nope(a)
        copy_lat(b, 0)
        squares(a, 0, 4)
        copy_lat(b, 1)
        inv_root(a, 0, 4)
        copy_v(a, 0)
        store_v(a, 0, 1)
        squares(a, 4, 8)
        copy_x(c, 0)
        copy_x(c, 1)
        scale_vector(a - 1, 0, 8)
        store_k(a - 1)
        quant_x(c)
        quant_lat(b)
        scale_vector(a, 0, 4)
        store_k(a, 0, 1)
        rope_products(b)
        rope_add(b)
        copy_v(a, 1)
        store_v(a, 1, 2)
        mm_lat(c, 0)
        mm_v(b, 0)
        mm_rope(c, 0, PAIR, ps_two, "xt")
        mm_nope(b)
        mm_lat(c, 1)
        mm_v(b, 1)
        copy_lat(c, 0)
        inv_root(a, 4, 8)
        copy_v(b, 0)
        store_v(b, 0, 1)
        copy_nope(b)
        copy_lat(c, 1)
        rope_products(c)
        copy_v(b, 1, vcopy)
        store_v(b, 1, 2)
        quant_lat(c)
        scale_vector(a, 4, 8)
        store_k(a, 1, 2)
        rope_add(c, 0, PAIR, nc.vector)
        mm_nope(c)
        mm_v(c, 0)
        mm_v(c, 1)
        squares(b, 0, 6)
        inv_root(b, 0, 4)
        squares(b, 6, 8)
        scale_vector(b, 0, 4)
        store_k(b, 0, 1)
        copy_nope(c)
        inv_root(b, 4, 8)
        copy_v(c, 0, vcopy)
        store_v(c, 0, 1)
        scale_vector(b, 4, 8)
        store_k(b, 1, 2)
        squares(c, 0, 6)
        copy_v(c, 1, vcopy)
        store_v(c, 1, 2)
        inv_root(c, 0, 4)
        squares_vector(c, 7, 8)
        squares(c, 6, 7)
        scale_vector(c, 0, 4)
        store_k(c, 0, 1)
        inv_root(c, 4, 8)
        scale_vector(c, 4, 8)
        store_k(c, 1, 2)
